import numpy as np
import ml_dtypes


def mxq(x, axis, fmt="e4m3"):
    dtype, down = {"e4m3": (ml_dtypes.float8_e4m3fn, 7), "e5m2": (ml_dtypes.float8_e5m2, 14)}[fmt]
    v = np.moveaxis(np.asarray(x, np.float32).astype(ml_dtypes.bfloat16).astype(np.float64), axis, -1)
    blocks = v.reshape(v.shape[:-1] + (-1, 32))
    amax = np.abs(blocks).max(-1, keepdims=True)
    byte = np.maximum(np.where(amax > 0, np.frexp(amax)[1] - 1 + 127, 0) - down, 1)
    scale = np.exp2(byte - 127.0)
    codes = (blocks / scale).astype(np.float32).astype(dtype).astype(np.float64)
    return np.moveaxis((codes * scale).reshape(v.shape), -1, axis)


WIDE = False


def mx_kscale(k):
    if not WIDE:
        return np.ones(k)
    levels = np.array([10, -10, 5, -5, 0])
    if k % 512:
        return np.exp2(np.random.permutation(np.resize(levels, k // 32))).repeat(32)
    a = np.empty((k // 512, 16))
    for p in range(k // 512):
        a[p, :8] = np.random.permutation(np.resize(levels, 8))
        for g in range(8):
            far = levels[np.abs(levels - a[p, g]) >= 10]
            a[p, g + 8] = far[np.random.randint(len(far))]
    return np.exp2(a.ravel()).repeat(32)


BF16 = ml_dtypes.bfloat16


def bf(x):
    return np.asarray(x, np.float32).astype(BF16)


def f64(x):
    return np.asarray(x).astype(np.float64)


E2M1 = np.array([0.0, 0.5, 1.0, 1.5, 2.0, 3.0, 4.0, 6.0, -0.0, -0.5, -1.0, -1.5, -2.0, -3.0, -4.0, -6.0])


def pack_weight(w, fmt):
    k, n = w.shape
    w = f64(bf(w)).reshape(k // 32, 32, n)
    amax = np.abs(w).max(1)
    if fmt == "e4m3":
        byte = np.frexp(amax)[1] - 1 + 127 - 7
    else:
        mant, ex = np.frexp(amax / 6.0)
        byte = np.where(mant > 0.5, ex, ex - 1) + 127
    byte = np.clip(np.where(amax > 0, byte, 1), 1, 254)
    scaled = (w * np.exp2(127.0 - byte)[:, None, :]).reshape(k, n).astype(np.float32)
    by_word = np.ascontiguousarray(scaled.reshape(k // 512, 128, 4, n).transpose(0, 1, 3, 2))
    if fmt == "e4m3":
        words = by_word.astype(ml_dtypes.float8_e4m3fn).view(np.uint8)
    else:
        c = by_word.astype(ml_dtypes.float4_e2m1fn).view(np.uint8) & 0xF
        words = c[..., 0::2] | (c[..., 1::2] << 4)
    return np.ascontiguousarray(words), np.ascontiguousarray(byte.astype(np.uint8).reshape(k // 512, 16, n))


def unpack_weight(words, scales, fmt):
    g, p, n, _ = words.shape
    if fmt == "e4m3":
        vals = np.ascontiguousarray(words).view(ml_dtypes.float8_e4m3fn).astype(np.float64)
    else:
        nib = np.empty((g, p, n, 4), np.uint8)
        nib[..., 0::2] = words & 0xF
        nib[..., 1::2] = words >> 4
        vals = E2M1[nib]
    vals = vals * np.repeat(np.exp2(scales.astype(np.float64) - 127.0), 8, axis=1)[..., None]
    return vals.transpose(0, 1, 3, 2).reshape(g * 512, n)
def pack4(w):
    words, scales = pack_weight(w, "e2m1")
    return words.reshape(words.shape[0], 128, -1), scales


def unpack4(words, scales):
    return unpack_weight(words.reshape(words.shape[0], 128, -1, 2), scales, "e2m1")


B, S, D, QR, KR, H, NOPE, ROPE, VD = 2, 2048, 1024, 1536, 512, 2, 128, 64, 128
EPS = 1e-6
THETA = 10000.0
LAT = 3.0 * np.sqrt(EPS)


def rmsnorm(x, w):
    var = np.mean(x * x, axis=-1, keepdims=True)
    return w * (x * (1.0 / np.sqrt(var + EPS)))


def rope_cos_sin(seq_len):
    inv_freq = 1.0 / (THETA ** (f64(np.arange(0, ROPE, 2)) / ROPE))
    t = f64(np.arange(seq_len))
    freqs = np.outer(t, inv_freq)
    emb = np.concatenate([freqs, freqs], -1)
    return np.cos(emb), np.sin(emb)


def rotate_half(x):
    x1, x2 = x[..., : x.shape[-1] // 2], x[..., x.shape[-1] // 2 :]
    return np.concatenate([-x2, x1], axis=-1)


def draw0():
    s, t = mx_kscale(D), mx_kscale(KR)
    hidden_states = bf(np.random.standard_normal((B, S, D)) * s)
    kv_a_w_ckv = np.random.standard_normal((KR, D)) * LAT / np.sqrt(D) / s[None, :]
    kv_a_w_ckv_words, kv_a_w_ckv_scales = pack4(kv_a_w_ckv.T)
    k_pe_raw = bf(np.random.standard_normal((B, S, ROPE)))
    kv_a_ln_w = bf((1.0 + 0.1 * np.random.standard_normal(KR)) * t)
    kv_b_w = np.random.standard_normal((H * (NOPE + VD), KR)) / np.sqrt(KR) / t[None, :]
    kv_b_w_words, kv_b_w_scales = pack4(kv_b_w.T)
    return {"hidden_states": hidden_states,
            "kv_a_w_ckv_words": kv_a_w_ckv_words,
            "kv_a_w_ckv_scales": kv_a_w_ckv_scales,
            "k_pe_raw": k_pe_raw,
            "kv_a_ln_w": kv_a_ln_w,
            "kv_b_w_words": kv_b_w_words,
            "kv_b_w_scales": kv_b_w_scales}


def core(hidden_states, kv_a_w_ckv_words, kv_a_w_ckv_scales, k_pe_raw, kv_a_ln_w, kv_b_w_words, kv_b_w_scales):
    ckv = mxq(f64(hidden_states), 2, "e4m3") @ unpack4(kv_a_w_ckv_words, kv_a_w_ckv_scales)
    ckv_n = rmsnorm(ckv, f64(kv_a_ln_w))
    kv = mxq(ckv_n, 2, "e4m3") @ unpack4(kv_b_w_words, kv_b_w_scales)
    kv = kv.reshape(B, S, H, NOPE + VD).transpose(0, 2, 1, 3)
    k_nope, v = kv[..., :NOPE], kv[..., NOPE:]
    k_pe = f64(k_pe_raw).reshape(B, 1, S, ROPE)
    cos, sin = rope_cos_sin(S)
    cos, sin = cos[None, None], sin[None, None]
    k_pe = k_pe * cos + rotate_half(k_pe) * sin
    key_s = np.concatenate([k_nope, np.broadcast_to(k_pe, (B, H, S, ROPE))], -1)
    return key_s, v


def e4m3fn_bytes(y):
    return np.clip(np.asarray(y, np.float64), -448.0, 448.0).astype(np.float32).astype(ml_dtypes.float8_e4m3fn).view(np.uint8)


def e4m3fn_values(b):
    return np.asarray(b, np.uint8).view(ml_dtypes.float8_e4m3fn).astype(np.float64)


def setup_inputs():
    d = draw0()
    x0 = np.asarray(d['hidden_states']).astype(np.float64)
    s = (np.max(np.abs(x0), axis=(0, 1), keepdims=True) / 448.0).astype(np.float32)
    out = {}
    for k, v in d.items():
        if k == 'hidden_states':
            out['hidden_states_bytes'] = e4m3fn_bytes(x0 / s.astype(np.float64))
            out['hidden_states_scale'] = s
        else:
            out[k] = v
    return out


def reference(hidden_states_bytes, hidden_states_scale, kv_a_w_ckv_words, kv_a_w_ckv_scales, k_pe_raw, kv_a_ln_w, kv_b_w_words, kv_b_w_scales):
    return core(e4m3fn_values(hidden_states_bytes) * hidden_states_scale.astype(np.float64), kv_a_w_ckv_words, kv_a_w_ckv_scales, k_pe_raw, kv_a_ln_w, kv_b_w_words, kv_b_w_scales)

@@ -1,0 +1,280 @@
+import math
+from contextlib import ExitStack
+
+import concourse.mybir as mybir
+from concourse.masks import make_identity
+
+B, S, D, KR = 2, 2048, 1024, 512
+H, NOPE, ROPE, VD = 2, 128, 64, 128
+EPS = 1e-6
+THETA = 10000.0
+FLOPS = 2 * B * S * (D * KR + KR * H * (NOPE + VD))
+
+F32 = mybir.dt.float32
+BF16 = mybir.dt.bfloat16
+I32 = mybir.dt.int32
+U32 = mybir.dt.uint32
+U8 = mybir.dt.uint8
+FP8 = mybir.dt.float8_e4m3fn
+FP8X4 = mybir.dt.float8_e4m3fn_x4
+FP4X4 = mybir.dt.float4_e2m1fn_x4
+ACT = mybir.ActivationFunctionType
+ALU = mybir.AluOpType
+
+P = 128
+RUN = S // P
+PAIRS = B * RUN // 2
+SLOT = NOPE + ROPE
+
+
+def tile_modelnew_pb_t_w4_kernel(
+    tc, x_bytes, x_scale, w1_words, w1_scales, k_pe_raw, ln_w, w2_words, w2_scales, key_out, v_out
+):
+    nc = tc.nc
+    with ExitStack() as ctx:
+        keep = ctx.enter_context(tc.tile_pool(name="keep", bufs=1))
+        work = ctx.enter_context(tc.tile_pool(name="work", bufs=2))
+        psum = ctx.enter_context(tc.psum_pool(name="psum", bufs=1))
+        ctx.enter_context(tc.manual_schedule())
+
+        xby = [keep.tile([P, RUN, D], U8, name=f"xby{b}") for b in range(B)]
+        w1 = keep.tile([P, 2, 2 * KR], U8, name="w1", align_bytes=64)
+        w1s = keep.tile([P, 2, KR], U8, name="w1s", align_bytes=64)
+        w2 = keep.tile([P, 1, 2 * KR], U8, name="w2", align_bytes=64)
+        w2s = keep.tile([P, 1, KR], U8, name="w2s", align_bytes=64)
+        xs = keep.tile([P, 2, 1, 2, 2], F32, name="xs")
+        gain = keep.tile([P, KR], BF16, name="gain")
+        kp = keep.tile([P, B, RUN, ROPE], BF16, name="kp")
+
+        nc.vector.memset(w1s[:].rearrange("p g n -> p (g n)").bitcast(I32), 0)
+        nc.vector.memset(w2s[:].rearrange("p g n -> p (g n)").bitcast(I32), 0)
+        ident = keep.tile([P, P], F32, name="ident")
+        make_identity(nc, ident[:])
+        pos = keep.tile([P, RUN], F32, name="pos")
+        nc.gpsimd.iota(pos[:], [[1, RUN]], base=0, channel_multiplier=RUN, allow_small_or_imprecise_dtypes=True)
+
+        def load_x(b, i0, i1):
+            nc.sync.dma_start(
+                out=xby[b][:, i0:i1, :], in_=x_bytes[b].rearrange("(p i) k -> p i k", i=RUN)[:, i0:i1, :]
+            )
+
+        def load_scales(tile, dram):
+            for q in range(4):
+                nc.sync.dma_start(
+                    out=tile[32 * q : 32 * q + 4, :, :].bitcast(I32),
+                    in_=dram[:, 4 * q : 4 * q + 4, :].rearrange("g q n -> q g n").bitcast(I32),
+                )
+
+        load_x(0, 0, 2)
+        nc.gpsimd.dma_start(
+            out=xs[:].rearrange("p g o u e -> p (g o) (u e)"),
+            in_=x_scale.rearrange("a b (g p t) -> p (a b g) t", p=P, t=4),
+        )
+        nc.gpsimd.dma_start(out=gain[:], in_=ln_w.partition_broadcast(P))
+        for b in range(B):
+            nc.gpsimd.dma_start(out=kp[:, b], in_=k_pe_raw[b].rearrange("(p i) d -> p i d", i=RUN))
+        load_scales(w1s, w1_scales)
+        nc.sync.dma_start(out=w1[:], in_=w1_words.rearrange("g p n -> p g n"))
+        load_x(0, 2, 4)
+        load_x(0, 4, 8)
+        load_scales(w2s, w2_scales)
+        nc.sync.dma_start(out=w2[:], in_=w2_words.rearrange("g p n -> p g n"))
+        load_x(0, 8, 12)
+        load_x(0, 12, 16)
+        for i in range(0, RUN, 4):
+            load_x(1, i, i + 4)
+
+        freq = keep.tile([P, 1, ROPE // 2], F32, name="freq")
+        nc.vector.tensor_scalar(
+            out=freq[:, 0, 0:1], in0=pos[:, 0:1], scalar1=0.0, scalar2=1.0 / (2.0 * math.pi), op0=ALU.mult, op1=ALU.add
+        )
+        w = 1
+        while w < ROPE // 2:
+            nc.vector.tensor_scalar(
+                out=freq[:, 0, w : 2 * w], in0=freq[:, 0, 0:w], scalar1=THETA ** (-2.0 * w / ROPE), scalar2=None, op0=ALU.mult
+            )
+            w *= 2
+        turns = keep.tile([P, RUN, ROPE // 2], F32, name="turns")
+        whole = keep.tile([P, RUN, ROPE // 2], I32, name="whole")
+        part = keep.tile([P, RUN, ROPE // 2], F32, name="part")
+        mag = keep.tile([P, RUN, ROPE // 2], F32, name="mag")
+        cos = keep.tile([P, RUN, 1, ROPE // 2], F32, name="cos")
+        sin = keep.tile([P, RUN, 2, ROPE // 2], F32, name="sin")
+        nc.vector.tensor_tensor(
+            out=turns[:],
+            in0=pos[:].unsqueeze(2).to_broadcast([P, RUN, ROPE // 2]),
+            in1=freq[:].to_broadcast([P, RUN, ROPE // 2]),
+            op=ALU.mult,
+        )
+        nc.vector.tensor_copy(out=whole[:], in_=turns[:])
+        nc.vector.tensor_tensor(out=part[:], in0=turns[:], in1=whole[:], op=ALU.subtract)
+
+        def rope_tables():
+            nc.scalar.activation(out=sin[:, :, 0, :], in_=part[:], func=ACT.Sin, scale=-2.0 * math.pi)
+            nc.scalar.activation(out=sin[:, :, 1, :], in_=part[:], func=ACT.Sin, scale=2.0 * math.pi)
+            nc.scalar.activation(out=mag[:], in_=part[:], func=ACT.Abs)
+            nc.scalar.activation(
+                out=cos[:, :, 0, :], in_=mag[:], func=ACT.Sin, scale=-2.0 * math.pi, bias=0.5 * math.pi
+            )
+
+        sums = keep.tile([P, 2 * PAIRS], F32, name="sums")
+        rinv = keep.tile([P, 2 * PAIRS], F32, name="rinv")
+        live = {}
+
+        def place(k):
+            return k // (RUN // 2), 2 * (k % (RUN // 2))
+
+        def widen(k):
+            b, i = place(k)
+            xb = work.tile([P, 2 * D], BF16, name="xb", bufs=3)
+            nc.scalar.copy(out=xb[:], in_=xby[b][:, i : i + 2, :].rearrange("p i k -> p (i k)").bitcast(FP8))
+            live["xb", k] = xb
+
+        def turn_x(k, g):
+            words = live["xb", k][:].bitcast(F32)
+            xt = psum.tile([P, 2, 2 * P], F32, name="xt", bufs=2)
+            for j in range(2):
+                for u in range(2):
+                    c = j * (D // 2) + g * 256 + u
+                    nc.tensor.transpose(xt[:, u, j * P : (j + 1) * P], words[:, c : c + 255 : 2], ident[:])
+            live["xt", k, g] = xt
+
+        def scale_x(k, g):
+            if g == 0:
+                live["xg", k] = work.tile([P, 2, 2 * P, 4], BF16, name="xg", align_bytes=64)
+            xt = live.pop(("xt", k, g))
+            nc.vector.tensor_tensor(
+                out=live["xg", k][:, g].rearrange("p r (u e) -> p r u e", u=2),
+                in0=xt[:].rearrange("p u r -> p (u r)").bitcast(BF16).rearrange("p (u r e) -> p r u e", u=2, e=2),
+                in1=xs[:, g].to_broadcast([P, 2 * P, 2, 2]),
+                op=ALU.mult,
+            )
+
+        def quant_x(k):
+            xq = work.tile([P, 2, 2 * P], U32, name="xq", align_bytes=64)
+            xqs = work.tile([P, 2, 2 * P], U8, name="xqs", align_bytes=64)
+            nc.vector.quantize_mx(
+                out=xq[:].rearrange("p g r -> p (g r)").bitcast(FP8X4),
+                scales=xqs[:].rearrange("p g r -> p (g r)"),
+                in_=live.pop(("xg", k))[:].rearrange("p g r t -> p (g r t)"),
+            )
+            live["xq", k] = (xq, xqs)
+
+        def down(k, j):
+            xq, xqs = live["xq", k]
+            ck = psum.tile([P, KR], F32, name="ck", bufs=3)
+            rows = slice(j * P, (j + 1) * P)
+            for g in range(2):
+                nc.tensor.matmul_mx(
+                    out=ck[:], lhsT=xq[:, g, rows].bitcast(FP8X4), lhsT_scale=xqs[:, g, rows],
+                    rhs=w1[:, g, :].bitcast(FP4X4), rhs_scale=w1s[:, g, :], start=(g == 0), stop=(g == 1),
+                )
+            live["ck", k, j] = ck
+
+        def squares(k, j):
+            junk = work.tile([P, KR], BF16, name="junk")
+            t = 2 * k + j
+            nc.scalar.activation(
+                out=junk[:], in_=live["ck", k, j][:], func=ACT.Square, accum_out=sums[:, t : t + 1]
+            )
+
+        def inverse(k):
+            t = slice(2 * k, 2 * k + 2)
+            nc.scalar.activation(
+                out=rinv[:, t], in_=sums[:, t], func=ACT.Abs_reciprocal_sqrt, scale=1.0 / KR, bias=EPS
+            )
+
+        def norm(k, j):
+            if j == 0:
+                live["nb", k] = work.tile([P, 2, KR], BF16, name="nb")
+            t = 2 * k + j
+            nc.vector.scalar_tensor_tensor(
+                out=live["nb", k][:, j], in0=live.pop(("ck", k, j))[:], scalar=rinv[:, t : t + 1], in1=gain[:],
+                op0=ALU.mult, op1=ALU.mult,
+            )
+
+        def turn_n(k, j):
+            if j == 0:
+                live["nt", k] = psum.tile([P, 2, 2 * P], F32, name="nt", bufs=1)
+            words = live["nb", k][:].rearrange("p j n -> p (j n)").bitcast(F32)
+            for u in range(2):
+                c = j * 256 + u
+                nc.tensor.transpose(live["nt", k][:, u, j * P : (j + 1) * P], words[:, c : c + 255 : 2], ident[:])
+
+        def empty_n(k):
+            ng = work.tile([P, 4 * 2 * P], BF16, name="ng", align_bytes=64)
+            nc.scalar.copy(
+                out=ng[:].bitcast(F32).rearrange("p (r u) -> p r u", u=2),
+                in_=live.pop(("nt", k))[:].rearrange("p u r -> p r u"),
+            )
+            live["ng", k] = ng
+
+        def quant_n(k):
+            nq = work.tile([P, 2 * P], U32, name="nq", align_bytes=64)
+            nqs = work.tile([P, 2 * P], U8, name="nqs", align_bytes=64)
+            nc.vector.quantize_mx(out=nq[:].bitcast(FP8X4), scales=nqs[:], in_=live.pop(("ng", k))[:])
+            live["nq", k] = (nq, nqs)
+
+        def up(k, j):
+            nq, nqs = live["nq", k]
+            kv = psum.tile([P, 4, P], F32, name="kv", bufs=2)
+            rows = slice(j * P, (j + 1) * P)
+            nc.tensor.matmul_mx(
+                out=kv[:].rearrange("p s d -> p (s d)"), lhsT=nq[:, rows].bitcast(FP8X4), lhsT_scale=nqs[:, rows],
+                rhs=w2[:, 0, :].bitcast(FP4X4), rhs_scale=w2s[:, 0, :], start=True, stop=True,
+            )
+            live["kv", k, j] = kv
+
+        def rope(k):
+            b, i = place(k)
+            res = work.tile([P, 2, 4, SLOT], F32, name="res", bufs=4)
+            live["res", k] = res
+            pe = kp[:, b, i : i + 2, :].rearrange("p i (c j) -> p i c j", c=2)
+            m1 = work.tile([P, 2, 2, ROPE // 2], F32, name="m1")
+            m2 = work.tile([P, 2, 2, ROPE // 2], F32, name="m2")
+            nc.gpsimd.tensor_tensor(
+                out=m1[:], in0=pe, in1=cos[:, i : i + 2].to_broadcast([P, 2, 2, ROPE // 2]), op=ALU.mult
+            )
+            for c in range(2):
+                nc.gpsimd.tensor_tensor(
+                    out=m2[:, :, c, :], in0=pe[:, :, 1 - c, :], in1=sin[:, i : i + 2, c, :], op=ALU.mult
+                )
+            nc.gpsimd.tensor_tensor(
+                out=res[:, :, 0, NOPE:SLOT], in0=m1[:].rearrange("p i c j -> p i (c j)"),
+                in1=m2[:].rearrange("p i c j -> p i (c j)"), op=ALU.add,
+            )
+            nc.gpsimd.tensor_scalar(
+                out=res[:, :, 2, NOPE:SLOT], in0=res[:, :, 0, NOPE:SLOT], scalar1=1.0, scalar2=0.0,
+                op0=ALU.mult, op1=ALU.add,
+            )
+
+        def empty_kv(k, j):
+            nc.scalar.copy(out=live["res", k][:, j, :, 0:NOPE], in_=live.pop(("kv", k, j))[:])
+
+        def store(k):
+            b, i = place(k)
+            res = live.pop(("res", k))
+            for h in range(H):
+                nc.sync.dma_start(
+                    out=key_out[b, h].rearrange("(p i) d -> p i d", i=RUN)[:, i : i + 2, :], in_=res[:, :, 2 * h, :]
+                )
+                nc.sync.dma_start(
+                    out=v_out[b, h].rearrange("(p i) d -> p i d", i=RUN)[:, i : i + 2, :],
+                    in_=res[:, :, 2 * h + 1, 0:VD],
+                )
+
+        def both(f):
+            return lambda k: (f(k, 0), f(k, 1))
+
+        steps = [
+            (0, widen), (4, empty_n), (2, quant_x), (3, both(norm)), (5, both(up)), (2, both(down)),
+            (3, rope), (5, both(empty_kv)), (5, store), (3, both(turn_n)),
+            (1, lambda k: scale_x(k, 0)), (4, quant_n), (1, lambda k: scale_x(k, 1)),
+            (0, both(turn_x)), (2, both(squares)), (2, inverse),
+        ]
+        for it in range(PAIRS + 5):
+            for lag, stage in steps:
+                if 0 <= it - lag < PAIRS:
+                    stage(it - lag)
+            if it == 0:
+                rope_tables()

@@ -23,6 +23,7 @@ ALU = mybir.AluOpType
 
 P = 128
 RUN = S // P
+LATE = 3
 PAIRS = B * RUN // 2
 SLOT = NOPE + ROPE
 
@@ -43,6 +44,7 @@ def tile_modelnew_pb_t_w4_kernel(
         w2 = keep.tile([P, 1, 2 * KR], U8, name="w2", align_bytes=64)
         w2s = keep.tile([P, 1, KR], U8, name="w2s", align_bytes=64)
         xs = keep.tile([P, 2, 1, 2, 2], F32, name="xs")
+        sbc = keep.tile([P, D], F32, name="sbc")
         gain = keep.tile([P, KR], BF16, name="gain")
         kp = keep.tile([P, B, RUN, ROPE], BF16, name="kp")
 
@@ -65,11 +67,13 @@ def tile_modelnew_pb_t_w4_kernel(
                     in_=dram[:, 4 * q : 4 * q + 4, :].rearrange("g q n -> q g n").bitcast(I32),
                 )
 
-        load_x(0, 0, 2)
+        load_x(0, 0, 1)
+        load_x(0, 1, 2)
         nc.gpsimd.dma_start(
             out=xs[:].rearrange("p g o u e -> p (g o) (u e)"),
             in_=x_scale.rearrange("a b (g p t) -> p (a b g) t", p=P, t=4),
         )
+        nc.gpsimd.dma_start(out=sbc[:], in_=x_scale.rearrange("a b k -> (a b k)").partition_broadcast(P))
         nc.gpsimd.dma_start(out=gain[:], in_=ln_w.partition_broadcast(P))
         for b in range(B):
             nc.gpsimd.dma_start(out=kp[:, b], in_=k_pe_raw[b].rearrange("(p i) d -> p i d", i=RUN))
@@ -124,31 +128,49 @@ def tile_modelnew_pb_t_w4_kernel(
         def place(k):
             return k // (RUN // 2), 2 * (k % (RUN // 2))
 
-        def widen(k):
+        def raw(k, j):
             b, i = place(k)
-            xb = work.tile([P, 2 * D], BF16, name="xb", bufs=3)
-            nc.scalar.copy(out=xb[:], in_=xby[b][:, i : i + 2, :].rearrange("p i k -> p (i k)").bitcast(FP8))
-            live["xb", k] = xb
+            return xby[b][:, i + j, :].bitcast(FP8)
 
-        def turn_x(k, g):
-            words = live["xb", k][:].bitcast(F32)
-            xt = psum.tile([P, 2, 2 * P], F32, name="xt", bufs=2)
-            for j in range(2):
+        def first(k, j):
+            if j == 0:
+                live["xb", k] = work.tile([P, 2, D], BF16, name="xb", bufs=3)
+            xb = live["xb", k][:, j]
+            if k == 0:
+                nc.vector.tensor_copy(out=xb, in_=raw(k, j))
+            elif k < LATE:
+                nc.scalar.copy(out=xb, in_=raw(k, j))
+            else:
+                nc.vector.tensor_tensor(out=xb, in0=raw(k, j), in1=sbc[:], op=ALU.mult)
+
+        def turn_x(k, a):
+            words = live["xb", k][:].rearrange("p j n -> p (j n)").bitcast(F32)
+            xt = psum.tile([P, 2, 2, P], F32, name="xt", bufs=2)
+            for o in range(2):
+                j, g = (o, a) if k < LATE else (a, o)
                 for u in range(2):
                     c = j * (D // 2) + g * 256 + u
-                    nc.tensor.transpose(xt[:, u, j * P : (j + 1) * P], words[:, c : c + 255 : 2], ident[:])
-            live["xt", k, g] = xt
+                    out = xt[:, u, o] if k < LATE else xt[:, o, u]
+                    nc.tensor.transpose(out, words[:, c : c + 255 : 2], ident[:])
+            live["xt", k, a] = xt
 
-        def scale_x(k, g):
-            if g == 0:
+        def second(k, a):
+            if a == 0:
                 live["xg", k] = work.tile([P, 2, 2 * P, 4], BF16, name="xg", align_bytes=64)
-            xt = live.pop(("xt", k, g))
-            nc.vector.tensor_tensor(
-                out=live["xg", k][:, g].rearrange("p r (u e) -> p r u e", u=2),
-                in0=xt[:].rearrange("p u r -> p (u r)").bitcast(BF16).rearrange("p (u r e) -> p r u e", u=2, e=2),
-                in1=xs[:, g].to_broadcast([P, 2 * P, 2, 2]),
-                op=ALU.mult,
-            )
+            xt = live.pop(("xt", k, a))
+            xg = live["xg", k]
+            if k < LATE:
+                nc.vector.tensor_tensor(
+                    out=xg[:, a].rearrange("p r (u e) -> p r u e", u=2),
+                    in0=xt[:].rearrange("p u j r -> p (u j r)").bitcast(BF16).rearrange("p (u r e) -> p r u e", u=2, e=2),
+                    in1=xs[:, a].to_broadcast([P, 2 * P, 2, 2]),
+                    op=ALU.mult,
+                )
+            else:
+                nc.scalar.copy(
+                    out=xg[:, a].rearrange("p r t -> p (r t)").bitcast(F32).rearrange("p (g r u) -> p g r u", g=2, u=2),
+                    in_=xt[:].rearrange("p g u r -> p g r u"),
+                )
 
         def quant_x(k):
             xq = work.tile([P, 2, 2 * P], U32, name="xq", align_bytes=64)
@@ -163,10 +185,11 @@ def tile_modelnew_pb_t_w4_kernel(
         def down(k, j):
             xq, xqs = live["xq", k]
             ck = psum.tile([P, KR], F32, name="ck", bufs=3)
-            rows = slice(j * P, (j + 1) * P)
             for g in range(2):
+                a, o = (g, j) if k < LATE else (j, g)
+                rows = slice(o * P, (o + 1) * P)
                 nc.tensor.matmul_mx(
-                    out=ck[:], lhsT=xq[:, g, rows].bitcast(FP8X4), lhsT_scale=xqs[:, g, rows],
+                    out=ck[:], lhsT=xq[:, a, rows].bitcast(FP8X4), lhsT_scale=xqs[:, a, rows],
                     rhs=w1[:, g, :].bitcast(FP4X4), rhs_scale=w1s[:, g, :], start=(g == 0), stop=(g == 1),
                 )
             live["ck", k, j] = ck
@@ -225,56 +248,53 @@ def tile_modelnew_pb_t_w4_kernel(
             )
             live["kv", k, j] = kv
 
-        def rope(k):
-            b, i = place(k)
-            res = work.tile([P, 2, 4, SLOT], F32, name="res", bufs=4)
-            live["res", k] = res
-            pe = kp[:, b, i : i + 2, :].rearrange("p i (c j) -> p i c j", c=2)
-            m1 = work.tile([P, 2, 2, ROPE // 2], F32, name="m1")
-            m2 = work.tile([P, 2, 2, ROPE // 2], F32, name="m2")
+        def rope(q):
+            b, i = place(2 * q)
+            res = keep.tile([P, 4, 4, SLOT], F32, name=f"res{q}")
+            live["res", q] = res
+            pe = kp[:, b, i : i + 4, :].rearrange("p i (c j) -> p i c j", c=2)
+            m1 = work.tile([P, 4, 2, ROPE // 2], F32, name="m1")
+            m2 = work.tile([P, 4, 2, ROPE // 2], F32, name="m2")
             nc.gpsimd.tensor_tensor(
-                out=m1[:], in0=pe, in1=cos[:, i : i + 2].to_broadcast([P, 2, 2, ROPE // 2]), op=ALU.mult
+                out=m1[:], in0=pe, in1=cos[:, i : i + 4].to_broadcast([P, 4, 2, ROPE // 2]), op=ALU.mult
             )
             for c in range(2):
                 nc.gpsimd.tensor_tensor(
-                    out=m2[:, :, c, :], in0=pe[:, :, 1 - c, :], in1=sin[:, i : i + 2, c, :], op=ALU.mult
+                    out=m2[:, :, c, :], in0=pe[:, :, 1 - c, :], in1=sin[:, i : i + 4, c, :], op=ALU.mult
                 )
             nc.gpsimd.tensor_tensor(
                 out=res[:, :, 0, NOPE:SLOT], in0=m1[:].rearrange("p i c j -> p i (c j)"),
                 in1=m2[:].rearrange("p i c j -> p i (c j)"), op=ALU.add,
             )
-            nc.gpsimd.tensor_scalar(
-                out=res[:, :, 2, NOPE:SLOT], in0=res[:, :, 0, NOPE:SLOT], scalar1=1.0, scalar2=0.0,
-                op0=ALU.mult, op1=ALU.add,
-            )
 
         def empty_kv(k, j):
-            nc.scalar.copy(out=live["res", k][:, j, :, 0:NOPE], in_=live.pop(("kv", k, j))[:])
+            nc.scalar.copy(out=live["res", k // 2][:, 2 * (k % 2) + j, :, 0:NOPE], in_=live.pop(("kv", k, j))[:])
 
         def store(k):
             b, i = place(k)
-            res = live.pop(("res", k))
+            c = 2 * (k % 2)
+            res = live["res", k // 2][:, c : c + 2]
+            keys = [key_out[b, h].rearrange("(p i) d -> p i d", i=RUN)[:, i : i + 2, :] for h in range(H)]
+            nc.sync.dma_start(out=keys[0], in_=res[:, :, 0, :])
+            nc.sync.dma_start(out=keys[1][:, :, NOPE:SLOT], in_=res[:, :, 0, NOPE:SLOT])
+            nc.sync.dma_start(out=keys[1][:, :, 0:NOPE], in_=res[:, :, 2, 0:NOPE])
             for h in range(H):
-                nc.sync.dma_start(
-                    out=key_out[b, h].rearrange("(p i) d -> p i d", i=RUN)[:, i : i + 2, :], in_=res[:, :, 2 * h, :]
-                )
                 nc.sync.dma_start(
                     out=v_out[b, h].rearrange("(p i) d -> p i d", i=RUN)[:, i : i + 2, :],
                     in_=res[:, :, 2 * h + 1, 0:VD],
                 )
 
-        def both(f):
-            return lambda k: (f(k, 0), f(k, 1))
-
         steps = [
-            (0, widen), (4, empty_n), (2, quant_x), (3, both(norm)), (5, both(up)), (2, both(down)),
-            (3, rope), (5, both(empty_kv)), (5, store), (3, both(turn_n)),
-            (1, lambda k: scale_x(k, 0)), (4, quant_n), (1, lambda k: scale_x(k, 1)),
-            (0, both(turn_x)), (2, both(squares)), (2, inverse),
+            (quant_x, None, 2), (inverse, None, 3), (down, 0, 2), (empty_n, None, 4), (norm, 0, 3), (down, 1, 2),
+            (empty_kv, 0, 5), (first, 0, 0), (up, 1, 5), (norm, 1, 3), (turn_n, 0, 3), (second, 0, 1), (quant_n, None, 4),
+            (second, 1, 1), (turn_n, 1, 3), (first, 1, 0), (up, 0, 4), (squares, 0, 2), (squares, 1, 2),
+            (empty_kv, 1, 5), (store, None, 5), (turn_x, 0, 0), (turn_x, 1, 0),
         ]
+        rope_tables()
+        for q in range(PAIRS // 2):
+            rope(q)
         for it in range(PAIRS + 5):
-            for lag, stage in steps:
-                if 0 <= it - lag < PAIRS:
-                    stage(it - lag)
-            if it == 0:
-                rope_tables()
+            for stage, j, lag in steps:
+                k = it - lag
+                if 0 <= k < PAIRS:
+                    stage(k) if j is None else stage(k, j)

@@ -23,7 +23,6 @@ ALU = mybir.AluOpType
 
 P = 128
 RUN = S // P
-LATE = 3
 PAIRS = B * RUN // 2
 SLOT = NOPE + ROPE
 
@@ -44,7 +43,6 @@ def tile_modelnew_pb_t_w4_kernel(
         w2 = keep.tile([P, 1, 2 * KR], U8, name="w2", align_bytes=64)
         w2s = keep.tile([P, 1, KR], U8, name="w2s", align_bytes=64)
         xs = keep.tile([P, 2, 1, 2, 2], F32, name="xs")
-        sbc = keep.tile([P, D], F32, name="sbc")
         gain = keep.tile([P, KR], BF16, name="gain")
         kp = keep.tile([P, B, RUN, ROPE], BF16, name="kp")
 
@@ -68,12 +66,11 @@ def tile_modelnew_pb_t_w4_kernel(
                 )
 
         load_x(0, 0, 1)
-        load_x(0, 1, 2)
-        nc.gpsimd.dma_start(
+        nc.sync.dma_start(
             out=xs[:].rearrange("p g o u e -> p (g o) (u e)"),
             in_=x_scale.rearrange("a b (g p t) -> p (a b g) t", p=P, t=4),
         )
-        nc.gpsimd.dma_start(out=sbc[:], in_=x_scale.rearrange("a b k -> (a b k)").partition_broadcast(P))
+        load_x(0, 1, 2)
         nc.gpsimd.dma_start(out=gain[:], in_=ln_w.partition_broadcast(P))
         for b in range(B):
             nc.gpsimd.dma_start(out=kp[:, b], in_=k_pe_raw[b].rearrange("(p i) d -> p i d", i=RUN))
@@ -132,45 +129,40 @@ def tile_modelnew_pb_t_w4_kernel(
             b, i = place(k)
             return xby[b][:, i + j, :].bitcast(FP8)
 
-        def first(k, j):
-            if j == 0:
-                live["xb", k] = work.tile([P, 2, D], BF16, name="xb", bufs=3)
-            xb = live["xb", k][:, j]
-            if k == 0:
-                nc.vector.tensor_copy(out=xb, in_=raw(k, j))
-            elif k < LATE:
-                nc.scalar.copy(out=xb, in_=raw(k, j))
-            else:
-                nc.vector.tensor_tensor(out=xb, in0=raw(k, j), in1=sbc[:], op=ALU.mult)
+        def widen_early(k):
+            live["xb", k] = work.tile([P, 2, D], BF16, name="xb", bufs=3)
+            if k % 2 == 0 and k > 0:
+                nc.scalar.copy(out=live["xb", k][:, 0], in_=raw(k, 0))
 
-        def turn_x(k, a):
+        def widen_vector(k):
+            if k % 2 == 1 or k == 0:
+                nc.vector.tensor_copy(out=live["xb", k][:, 0], in_=raw(k, 0))
+            if k == 0:
+                nc.vector.tensor_copy(out=live["xb", k][:, 1], in_=raw(k, 1))
+
+        def widen_late(k):
+            if k > 0:
+                nc.scalar.copy(out=live["xb", k][:, 1], in_=raw(k, 1))
+
+        def turn_x(k, g):
             words = live["xb", k][:].rearrange("p j n -> p (j n)").bitcast(F32)
             xt = psum.tile([P, 2, 2, P], F32, name="xt", bufs=2)
-            for o in range(2):
-                j, g = (o, a) if k < LATE else (a, o)
+            for j in range(2):
                 for u in range(2):
                     c = j * (D // 2) + g * 256 + u
-                    out = xt[:, u, o] if k < LATE else xt[:, o, u]
-                    nc.tensor.transpose(out, words[:, c : c + 255 : 2], ident[:])
-            live["xt", k, a] = xt
+                    nc.tensor.transpose(xt[:, u, j], words[:, c : c + 255 : 2], ident[:])
+            live["xt", k, g] = xt
 
-        def second(k, a):
-            if a == 0:
+        def scale_x(k, g):
+            if g == 0:
                 live["xg", k] = work.tile([P, 2, 2 * P, 4], BF16, name="xg", align_bytes=64)
-            xt = live.pop(("xt", k, a))
-            xg = live["xg", k]
-            if k < LATE:
-                nc.vector.tensor_tensor(
-                    out=xg[:, a].rearrange("p r (u e) -> p r u e", u=2),
-                    in0=xt[:].rearrange("p u j r -> p (u j r)").bitcast(BF16).rearrange("p (u r e) -> p r u e", u=2, e=2),
-                    in1=xs[:, a].to_broadcast([P, 2 * P, 2, 2]),
-                    op=ALU.mult,
-                )
-            else:
-                nc.scalar.copy(
-                    out=xg[:, a].rearrange("p r t -> p (r t)").bitcast(F32).rearrange("p (g r u) -> p g r u", g=2, u=2),
-                    in_=xt[:].rearrange("p g u r -> p g r u"),
-                )
+            xt = live.pop(("xt", k, g))
+            nc.vector.tensor_tensor(
+                out=live["xg", k][:, g].rearrange("p r (u e) -> p r u e", u=2),
+                in0=xt[:].rearrange("p u j r -> p (u j r)").bitcast(BF16).rearrange("p (u r e) -> p r u e", u=2, e=2),
+                in1=xs[:, g].to_broadcast([P, 2 * P, 2, 2]),
+                op=ALU.mult,
+            )
 
         def quant_x(k):
             xq = work.tile([P, 2, 2 * P], U32, name="xq", align_bytes=64)
@@ -185,11 +177,10 @@ def tile_modelnew_pb_t_w4_kernel(
         def down(k, j):
             xq, xqs = live["xq", k]
             ck = psum.tile([P, KR], F32, name="ck", bufs=3)
+            rows = slice(j * P, (j + 1) * P)
             for g in range(2):
-                a, o = (g, j) if k < LATE else (j, g)
-                rows = slice(o * P, (o + 1) * P)
                 nc.tensor.matmul_mx(
-                    out=ck[:], lhsT=xq[:, a, rows].bitcast(FP8X4), lhsT_scale=xqs[:, a, rows],
+                    out=ck[:], lhsT=xq[:, g, rows].bitcast(FP8X4), lhsT_scale=xqs[:, g, rows],
                     rhs=w1[:, g, :].bitcast(FP4X4), rhs_scale=w1s[:, g, :], start=(g == 0), stop=(g == 1),
                 )
             live["ck", k, j] = ck
@@ -285,15 +276,15 @@ def tile_modelnew_pb_t_w4_kernel(
                 )
 
         steps = [
-            (quant_x, None, 2), (inverse, None, 3), (down, 0, 2), (empty_n, None, 4), (norm, 0, 3), (down, 1, 2),
-            (empty_kv, 0, 5), (first, 0, 0), (up, 1, 5), (norm, 1, 3), (turn_n, 0, 3), (second, 0, 1), (quant_n, None, 4),
-            (second, 1, 1), (turn_n, 1, 3), (first, 1, 0), (up, 0, 4), (squares, 0, 2), (squares, 1, 2),
-            (empty_kv, 1, 5), (store, None, 5), (turn_x, 0, 0), (turn_x, 1, 0),
+            (turn_n, 1, 4), (quant_x, None, 2), (widen_early, None, 0), (inverse, None, 3), (turn_x, 1, 1),
+            (widen_vector, None, 0), (empty_kv, 1, 6), (store, None, 6), (up, 0, 5), (scale_x, 0, 1), (widen_late, None, 0),
+            (norm, 0, 3), (down, 0, 2), (down, 1, 2), (scale_x, 1, 1), (up, 1, 5), (empty_n, None, 4), (turn_x, 0, 0),
+            (empty_kv, 0, 5), (turn_n, 0, 3), (norm, 1, 3), (squares, 0, 2), (squares, 1, 2), (quant_n, None, 4),
         ]
         rope_tables()
         for q in range(PAIRS // 2):
             rope(q)
-        for it in range(PAIRS + 5):
+        for it in range(PAIRS + 6):
             for stage, j, lag in steps:
                 k = it - lag
                 if 0 <= k < PAIRS:

@@ -23,7 +23,7 @@ ALU = mybir.AluOpType
 
 P = 128
 RUN = S // P
-PAIRS = B * RUN // 2
+TILES = B * RUN
 SLOT = NOPE + ROPE
 
 
@@ -38,15 +38,19 @@ def tile_modelnew_pb_t_w4_kernel(
         ctx.enter_context(tc.manual_schedule())
 
         xby = [keep.tile([P, RUN, D], U8, name=f"xby{b}") for b in range(B)]
+        w1_in = keep.tile([P, 2, 2 * KR], U8, name="w1_in", align_bytes=64)
+        w1s_in = keep.tile([P, 2, KR], U8, name="w1s_in", align_bytes=64)
         w1 = keep.tile([P, 2, 2 * KR], U8, name="w1", align_bytes=64)
         w1s = keep.tile([P, 2, KR], U8, name="w1s", align_bytes=64)
         w2 = keep.tile([P, 1, 2 * KR], U8, name="w2", align_bytes=64)
         w2s = keep.tile([P, 1, KR], U8, name="w2s", align_bytes=64)
-        xs = keep.tile([P, 2, 1, 2, 2], F32, name="xs")
-        gain = keep.tile([P, KR], BF16, name="gain")
+        xs = keep.tile([P, 2, 1, 4], F32, name="xs")
+        xsb = keep.tile([P, 2, P, 4], F32, name="xsb")
+        gain_in = keep.tile([P, KR], BF16, name="gain_in")
+        gain = keep.tile([P, 2, P, 2], BF16, name="gain")
         kp = keep.tile([P, B, RUN, ROPE], BF16, name="kp")
 
-        nc.vector.memset(w1s[:].rearrange("p g n -> p (g n)").bitcast(I32), 0)
+        nc.vector.memset(w1s_in[:].rearrange("p g n -> p (g n)").bitcast(I32), 0)
         nc.vector.memset(w2s[:].rearrange("p g n -> p (g n)").bitcast(I32), 0)
         ident = keep.tile([P, P], F32, name="ident")
         make_identity(nc, ident[:])
@@ -67,15 +71,15 @@ def tile_modelnew_pb_t_w4_kernel(
 
         load_x(0, 0, 1)
         nc.sync.dma_start(
-            out=xs[:].rearrange("p g o u e -> p (g o) (u e)"),
+            out=xs[:].rearrange("p g o t -> p (g o) t"),
             in_=x_scale.rearrange("a b (g p t) -> p (a b g) t", p=P, t=4),
         )
         load_x(0, 1, 2)
-        nc.gpsimd.dma_start(out=gain[:], in_=ln_w.partition_broadcast(P))
+        nc.gpsimd.dma_start(out=gain_in[:], in_=ln_w.partition_broadcast(P))
         for b in range(B):
             nc.gpsimd.dma_start(out=kp[:, b], in_=k_pe_raw[b].rearrange("(p i) d -> p i d", i=RUN))
-        load_scales(w1s, w1_scales)
-        nc.sync.dma_start(out=w1[:], in_=w1_words.rearrange("g p n -> p g n"))
+        load_scales(w1s_in, w1_scales)
+        nc.sync.dma_start(out=w1_in[:], in_=w1_words.rearrange("g p n -> p g n"))
         load_x(0, 2, 4)
         load_x(0, 4, 8)
         load_scales(w2s, w2_scales)
@@ -118,129 +122,121 @@ def tile_modelnew_pb_t_w4_kernel(
                 out=cos[:, :, 0, :], in_=mag[:], func=ACT.Sin, scale=-2.0 * math.pi, bias=0.5 * math.pi
             )
 
-        sums = keep.tile([P, 2 * PAIRS], F32, name="sums")
-        rinv = keep.tile([P, 2 * PAIRS], F32, name="rinv")
+        def permute_down():
+            nc.vector.tensor_copy(
+                out=w1[:].rearrange("p g n -> p (g n)").bitcast(I32).rearrange("p (g u q) -> p g u q", g=2, u=2),
+                in_=w1_in[:].rearrange("p g n -> p (g n)").bitcast(I32).rearrange("p (g q u) -> p g u q", g=2, u=2),
+            )
+            for g in range(2):
+                nc.vector.tensor_copy(
+                    out=w1s[:, g, :].rearrange("p (u q e) -> p u q e", u=2, e=2),
+                    in_=w1s_in[:, g, :].rearrange("p (q u e) -> p u q e", u=2, e=2),
+                )
+
+        sums = keep.tile([P, TILES], F32, name="sums")
+        rinv = keep.tile([P, TILES], F32, name="rinv")
         live = {}
 
-        def place(k):
-            return k // (RUN // 2), 2 * (k % (RUN // 2))
+        def raw(t):
+            return xby[t // RUN][:, t % RUN, :].bitcast(FP8)
 
-        def raw(k, j):
-            b, i = place(k)
-            return xby[b][:, i + j, :].bitcast(FP8)
+        def widen(t):
+            live["xb", t] = work.tile([P, D], BF16, name="xb", bufs=4)
+            if t < 2:
+                nc.vector.tensor_copy(out=live["xb", t][:], in_=raw(t))
+            else:
+                nc.scalar.copy(out=live["xb", t][:], in_=raw(t))
 
-        def widen_early(k):
-            live["xb", k] = work.tile([P, 2, D], BF16, name="xb", bufs=3)
-            if k % 2 == 0 and k > 0:
-                nc.scalar.copy(out=live["xb", k][:, 0], in_=raw(k, 0))
-
-        def widen_vector(k):
-            if k % 2 == 1 or k == 0:
-                nc.vector.tensor_copy(out=live["xb", k][:, 0], in_=raw(k, 0))
-            if k == 0:
-                nc.vector.tensor_copy(out=live["xb", k][:, 1], in_=raw(k, 1))
-
-        def widen_late(k):
-            if k > 0:
-                nc.scalar.copy(out=live["xb", k][:, 1], in_=raw(k, 1))
-
-        def turn_x(k, g):
-            words = live["xb", k][:].rearrange("p j n -> p (j n)").bitcast(F32)
+        def turn_x(t):
+            words = live.pop(("xb", t))[:].bitcast(F32)
             xt = psum.tile([P, 2, 2, P], F32, name="xt", bufs=2)
-            for j in range(2):
+            for g in range(2):
                 for u in range(2):
-                    c = j * (D // 2) + g * 256 + u
-                    nc.tensor.transpose(xt[:, u, j], words[:, c : c + 255 : 2], ident[:])
-            live["xt", k, g] = xt
+                    c = g * 256 + u
+                    nc.tensor.transpose(xt[:, u, g], words[:, c : c + 255 : 2], ident[:])
+            live["xt", t] = xt
 
-        def scale_x(k, g):
-            if g == 0:
-                live["xg", k] = work.tile([P, 2, 2 * P, 4], BF16, name="xg", align_bytes=64)
-            xt = live.pop(("xt", k, g))
+        def scale_x(t):
+            xg = work.tile([P, 2 * P, 4], BF16, name="xg", align_bytes=64, bufs=3)
             nc.vector.tensor_tensor(
-                out=live["xg", k][:, g].rearrange("p r (u e) -> p r u e", u=2),
-                in0=xt[:].rearrange("p u j r -> p (u j r)").bitcast(BF16).rearrange("p (u r e) -> p r u e", u=2, e=2),
-                in1=xs[:, g].to_broadcast([P, 2 * P, 2, 2]),
+                out=xg[:].rearrange("p m (u e) -> p m u e", u=2),
+                in0=live.pop(("xt", t))[:].rearrange("p u g r -> p (u g r)").bitcast(BF16).rearrange(
+                    "p (u m e) -> p m u e", u=2, e=2
+                ),
+                in1=xsb[:].rearrange("p g r (u e) -> p (g r) u e", u=2),
                 op=ALU.mult,
             )
+            live["xg", t] = xg
 
-        def quant_x(k):
-            xq = work.tile([P, 2, 2 * P], U32, name="xq", align_bytes=64)
-            xqs = work.tile([P, 2, 2 * P], U8, name="xqs", align_bytes=64)
+        def quant_x(t):
+            xq = work.tile([P, 2, P], U32, name="xq", align_bytes=64, bufs=3)
+            xqs = work.tile([P, 2, P], U8, name="xqs", align_bytes=64, bufs=3)
             nc.vector.quantize_mx(
                 out=xq[:].rearrange("p g r -> p (g r)").bitcast(FP8X4),
                 scales=xqs[:].rearrange("p g r -> p (g r)"),
-                in_=live.pop(("xg", k))[:].rearrange("p g r t -> p (g r t)"),
+                in_=live.pop(("xg", t))[:].rearrange("p m t -> p (m t)"),
             )
-            live["xq", k] = (xq, xqs)
+            live["xq", t] = (xq, xqs)
 
-        def down(k, j):
-            xq, xqs = live["xq", k]
+        def down(t):
+            xq, xqs = live.pop(("xq", t))
             ck = psum.tile([P, KR], F32, name="ck", bufs=3)
-            rows = slice(j * P, (j + 1) * P)
             for g in range(2):
                 nc.tensor.matmul_mx(
-                    out=ck[:], lhsT=xq[:, g, rows].bitcast(FP8X4), lhsT_scale=xqs[:, g, rows],
+                    out=ck[:], lhsT=xq[:, g, :].bitcast(FP8X4), lhsT_scale=xqs[:, g, :],
                     rhs=w1[:, g, :].bitcast(FP4X4), rhs_scale=w1s[:, g, :], start=(g == 0), stop=(g == 1),
                 )
-            live["ck", k, j] = ck
+            live["ck", t] = ck
 
-        def squares(k, j):
+        def squares(t):
             junk = work.tile([P, KR], BF16, name="junk")
-            t = 2 * k + j
+            nc.scalar.activation(out=junk[:], in_=live["ck", t][:], func=ACT.Square, accum_out=sums[:, t : t + 1])
+
+        def inverse(t):
             nc.scalar.activation(
-                out=junk[:], in_=live["ck", k, j][:], func=ACT.Square, accum_out=sums[:, t : t + 1]
+                out=rinv[:, t : t + 1], in_=sums[:, t : t + 1], func=ACT.Abs_reciprocal_sqrt, scale=1.0 / KR, bias=EPS
             )
 
-        def inverse(k):
-            t = slice(2 * k, 2 * k + 2)
-            nc.scalar.activation(
-                out=rinv[:, t], in_=sums[:, t], func=ACT.Abs_reciprocal_sqrt, scale=1.0 / KR, bias=EPS
-            )
-
-        def norm(k, j):
-            if j == 0:
-                live["nb", k] = work.tile([P, 2, KR], BF16, name="nb")
-            t = 2 * k + j
+        def norm(t):
+            nb = work.tile([P, KR], BF16, name="nb", bufs=3)
             nc.vector.scalar_tensor_tensor(
-                out=live["nb", k][:, j], in0=live.pop(("ck", k, j))[:], scalar=rinv[:, t : t + 1], in1=gain[:],
-                op0=ALU.mult, op1=ALU.mult,
+                out=nb[:], in0=live.pop(("ck", t))[:], scalar=rinv[:, t : t + 1],
+                in1=gain[:].rearrange("p u q e -> p (u q e)"), op0=ALU.mult, op1=ALU.mult,
             )
+            live["nb", t] = nb
 
-        def turn_n(k, j):
-            if j == 0:
-                live["nt", k] = psum.tile([P, 2, 2 * P], F32, name="nt", bufs=1)
-            words = live["nb", k][:].rearrange("p j n -> p (j n)").bitcast(F32)
+        def turn_n(t):
+            words = live.pop(("nb", t))[:].bitcast(F32)
+            nt = psum.tile([P, 2, P], F32, name="nt", bufs=1)
             for u in range(2):
-                c = j * 256 + u
-                nc.tensor.transpose(live["nt", k][:, u, j * P : (j + 1) * P], words[:, c : c + 255 : 2], ident[:])
+                nc.tensor.transpose(nt[:, u], words[:, u * P : (u + 1) * P], ident[:])
+            live["nt", t] = nt
 
-        def empty_n(k):
-            ng = work.tile([P, 4 * 2 * P], BF16, name="ng", align_bytes=64)
+        def empty_n(t):
+            ng = work.tile([P, 4 * P], BF16, name="ng", align_bytes=64, bufs=3)
             nc.scalar.copy(
                 out=ng[:].bitcast(F32).rearrange("p (r u) -> p r u", u=2),
-                in_=live.pop(("nt", k))[:].rearrange("p u r -> p r u"),
+                in_=live.pop(("nt", t))[:].rearrange("p u r -> p r u"),
             )
-            live["ng", k] = ng
+            live["ng", t] = ng
 
-        def quant_n(k):
-            nq = work.tile([P, 2 * P], U32, name="nq", align_bytes=64)
-            nqs = work.tile([P, 2 * P], U8, name="nqs", align_bytes=64)
-            nc.vector.quantize_mx(out=nq[:].bitcast(FP8X4), scales=nqs[:], in_=live.pop(("ng", k))[:])
-            live["nq", k] = (nq, nqs)
+        def quant_n(t):
+            nq = work.tile([P, P], U32, name="nq", align_bytes=64, bufs=3)
+            nqs = work.tile([P, P], U8, name="nqs", align_bytes=64, bufs=3)
+            nc.vector.quantize_mx(out=nq[:].bitcast(FP8X4), scales=nqs[:], in_=live.pop(("ng", t))[:])
+            live["nq", t] = (nq, nqs)
 
-        def up(k, j):
-            nq, nqs = live["nq", k]
+        def up(t):
+            nq, nqs = live.pop(("nq", t))
             kv = psum.tile([P, 4, P], F32, name="kv", bufs=2)
-            rows = slice(j * P, (j + 1) * P)
             nc.tensor.matmul_mx(
-                out=kv[:].rearrange("p s d -> p (s d)"), lhsT=nq[:, rows].bitcast(FP8X4), lhsT_scale=nqs[:, rows],
+                out=kv[:].rearrange("p s d -> p (s d)"), lhsT=nq[:].bitcast(FP8X4), lhsT_scale=nqs[:],
                 rhs=w2[:, 0, :].bitcast(FP4X4), rhs_scale=w2s[:, 0, :], start=True, stop=True,
             )
-            live["kv", k, j] = kv
+            live["kv", t] = kv
 
         def rope(q):
-            b, i = place(2 * q)
+            b, i = 4 * q // RUN, 4 * q % RUN
             res = keep.tile([P, 4, 4, SLOT], F32, name=f"res{q}")
             live["res", q] = res
             pe = kp[:, b, i : i + 4, :].rearrange("p i (c j) -> p i c j", c=2)
@@ -258,13 +254,14 @@ def tile_modelnew_pb_t_w4_kernel(
                 in1=m2[:].rearrange("p i c j -> p i (c j)"), op=ALU.add,
             )
 
-        def empty_kv(k, j):
-            nc.scalar.copy(out=live["res", k // 2][:, 2 * (k % 2) + j, :, 0:NOPE], in_=live.pop(("kv", k, j))[:])
+        def empty_kv(t):
+            nc.scalar.copy(out=live["res", t // 4][:, t % 4, :, 0:NOPE], in_=live.pop(("kv", t))[:])
 
-        def store(k):
-            b, i = place(k)
-            c = 2 * (k % 2)
-            res = live["res", k // 2][:, c : c + 2]
+        def store(t):
+            if t % 2 == 0:
+                return
+            b, i, c = t // RUN, t % RUN - 1, t % 4 - 1
+            res = live["res", t // 4][:, c : c + 2]
             keys = [key_out[b, h].rearrange("(p i) d -> p i d", i=RUN)[:, i : i + 2, :] for h in range(H)]
             nc.sync.dma_start(out=keys[0], in_=res[:, :, 0, :])
             nc.sync.dma_start(out=keys[1][:, :, NOPE:SLOT], in_=res[:, :, 0, NOPE:SLOT])
@@ -276,16 +273,22 @@ def tile_modelnew_pb_t_w4_kernel(
                 )
 
         steps = [
-            (turn_n, 1, 4), (quant_x, None, 2), (widen_early, None, 0), (inverse, None, 3), (turn_x, 1, 1),
-            (widen_vector, None, 0), (empty_kv, 1, 6), (store, None, 6), (up, 0, 5), (scale_x, 0, 1), (widen_late, None, 0),
-            (norm, 0, 3), (down, 0, 2), (down, 1, 2), (scale_x, 1, 1), (up, 1, 5), (empty_n, None, 4), (turn_x, 0, 0),
-            (empty_kv, 0, 5), (turn_n, 0, 3), (norm, 1, 3), (squares, 0, 2), (squares, 1, 2), (quant_n, None, 4),
+            (widen, 0), (turn_x, 1), (quant_x, 2), (empty_kv, 9), (store, 9), (squares, 4), (scale_x, 1), (empty_n, 6),
+            (up, 8), (inverse, 4), (down, 3), (norm, 4), (turn_n, 5), (quant_n, 6),
         ]
+        nc.gpsimd.tensor_scalar(
+            out=xsb[:], in0=xs[:].to_broadcast([P, 2, P, 4]), scalar1=1.0, scalar2=0.0, op0=ALU.mult, op1=ALU.add
+        )
+        nc.gpsimd.tensor_scalar(
+            out=gain[:], in0=gain_in[:].rearrange("p (q u e) -> p u q e", u=2, e=2), scalar1=1.0, scalar2=0.0,
+            op0=ALU.mult, op1=ALU.add,
+        )
         rope_tables()
-        for q in range(PAIRS // 2):
+        for q in range(TILES // 4):
             rope(q)
-        for it in range(PAIRS + 6):
-            for stage, j, lag in steps:
-                k = it - lag
-                if 0 <= k < PAIRS:
-                    stage(k) if j is None else stage(k, j)
+        for it in range(TILES + 9):
+            for stage, lag in steps:
+                if 0 <= it - lag < TILES:
+                    stage(it - lag)
+            if it == 1:
+                permute_down()

@@ -6,6 +6,7 @@ from concourse.masks import make_identity
 
 B, S, D, KR = 2, 2048, 1024, 512
 H, NOPE, ROPE, VD = 2, 128, 64, 128
+HALF = ROPE // 2
 EPS = 1e-6
 THETA = 10000.0
 FLOPS = 2 * B * S * (D * KR + KR * H * (NOPE + VD))
@@ -25,6 +26,11 @@ P = 128
 RUN = S // P
 TILES = B * RUN
 SLOT = NOPE + ROPE
+QUAD = 4
+
+
+def group_of(t):
+    return [t]
 
 
 def tile_modelnew_pb_t_w4_kernel(
@@ -33,29 +39,38 @@ def tile_modelnew_pb_t_w4_kernel(
     nc = tc.nc
     with ExitStack() as ctx:
         keep = ctx.enter_context(tc.tile_pool(name="keep", bufs=1))
-        work = ctx.enter_context(tc.tile_pool(name="work", bufs=2))
+        work = ctx.enter_context(tc.tile_pool(name="work", bufs=4))
         psum = ctx.enter_context(tc.psum_pool(name="psum", bufs=1))
         ctx.enter_context(tc.manual_schedule())
 
         xby = [keep.tile([P, RUN, D], U8, name=f"xby{b}") for b in range(B)]
-        w1_in = keep.tile([P, 2, 2 * KR], U8, name="w1_in", align_bytes=64)
-        w1s_in = keep.tile([P, 2, KR], U8, name="w1s_in", align_bytes=64)
+        xs = keep.tile([P, 2, 1, 4], F32, name="xs")
+        xsb = keep.tile([P, 2, P, 4], F32, name="xsb")
         w1 = keep.tile([P, 2, 2 * KR], U8, name="w1", align_bytes=64)
         w1s = keep.tile([P, 2, KR], U8, name="w1s", align_bytes=64)
         w2 = keep.tile([P, 1, 2 * KR], U8, name="w2", align_bytes=64)
         w2s = keep.tile([P, 1, KR], U8, name="w2s", align_bytes=64)
-        xs = keep.tile([P, 2, 1, 4], F32, name="xs")
-        xsb = keep.tile([P, 2, P, 4], F32, name="xsb")
-        gain_in = keep.tile([P, KR], BF16, name="gain_in")
-        gain = keep.tile([P, 2, P, 2], BF16, name="gain")
-        kp = keep.tile([P, B, RUN, ROPE], BF16, name="kp")
-
-        nc.vector.memset(w1s_in[:].rearrange("p g n -> p (g n)").bitcast(I32), 0)
-        nc.vector.memset(w2s[:].rearrange("p g n -> p (g n)").bitcast(I32), 0)
+        gain = keep.tile([P, KR], BF16, name="gain")
+        kp = keep.tile([P, B, RUN, 2, HALF], BF16, name="kp")
         ident = keep.tile([P, P], F32, name="ident")
-        make_identity(nc, ident[:])
-        pos = keep.tile([P, RUN], F32, name="pos")
-        nc.gpsimd.iota(pos[:], [[1, RUN]], base=0, channel_multiplier=RUN, allow_small_or_imprecise_dtypes=True)
+        zero = keep.tile([P, 1], F32, name="zero")
+        spare = keep.tile([P, 1], F32, name="spare")
+        pos = keep.tile([P, RUN, 1], F32, name="pos")
+        freq = keep.tile([P, 1, HALF], F32, name="freq")
+        turns = keep.tile([P, RUN, HALF], F32, name="turns")
+        whole = keep.tile([P, RUN, HALF], I32, name="whole")
+        part = keep.tile([P, RUN, HALF], F32, name="part")
+        sin = keep.tile([P, RUN, 1, HALF], F32, name="sin")
+        half_sin = keep.tile([P, RUN, 1, HALF], F32, name="half_sin")
+        cos = keep.tile([P, RUN, 1, HALF], F32, name="cos")
+        sums = keep.tile([P, TILES], F32, name="sums")
+        rinv = keep.tile([P, TILES], F32, name="rinv")
+        live = {}
+
+        nc.vector.memset(w1s[:].rearrange("p g n -> p (g n)").bitcast(I32), 0)
+        nc.vector.memset(zero[:], 0.0)
+        nc.vector.memset(w2s[:].rearrange("p g n -> p (g n)").bitcast(I32), 0)
+        nc.scalar.activation(out=spare[:], in_=zero[:], func=ACT.Sin)
 
         def load_x(b, i0, i1):
             nc.sync.dma_start(
@@ -69,86 +84,115 @@ def tile_modelnew_pb_t_w4_kernel(
                     in_=dram[:, 4 * q : 4 * q + 4, :].rearrange("g q n -> q g n").bitcast(I32),
                 )
 
+        def load_rope_key(b):
+            nc.sync.dma_start(
+                out=kp[:, b].rearrange("p i c j -> p i (c j)"), in_=k_pe_raw[b].rearrange("(p i) d -> p i d", i=RUN)
+            )
+
         load_x(0, 0, 1)
         nc.sync.dma_start(
             out=xs[:].rearrange("p g o t -> p (g o) t"),
             in_=x_scale.rearrange("a b (g p t) -> p (a b g) t", p=P, t=4),
         )
         load_x(0, 1, 2)
-        nc.gpsimd.dma_start(out=gain_in[:], in_=ln_w.partition_broadcast(P))
-        for b in range(B):
-            nc.gpsimd.dma_start(out=kp[:, b], in_=k_pe_raw[b].rearrange("(p i) d -> p i d", i=RUN))
-        load_scales(w1s_in, w1_scales)
-        nc.sync.dma_start(out=w1_in[:], in_=w1_words.rearrange("g p n -> p g n"))
+        nc.sync.dma_start(out=w1[:], in_=w1_words.rearrange("g p n -> p g n"))
+        load_scales(w1s, w1_scales)
         load_x(0, 2, 4)
         load_x(0, 4, 8)
+        nc.sync.dma_start(out=gain[:], in_=ln_w.partition_broadcast(P))
+        load_rope_key(0)
         load_scales(w2s, w2_scales)
         nc.sync.dma_start(out=w2[:], in_=w2_words.rearrange("g p n -> p g n"))
         load_x(0, 8, 12)
         load_x(0, 12, 16)
-        for i in range(0, RUN, 4):
+        load_x(1, 0, 4)
+        load_rope_key(1)
+        for i in range(4, RUN, 4):
             load_x(1, i, i + 4)
 
-        freq = keep.tile([P, 1, ROPE // 2], F32, name="freq")
-        nc.vector.tensor_scalar(
-            out=freq[:, 0, 0:1], in0=pos[:, 0:1], scalar1=0.0, scalar2=1.0 / (2.0 * math.pi), op0=ALU.mult, op1=ALU.add
+        make_identity(nc, ident[:])
+        nc.gpsimd.iota(
+            pos[:].rearrange("p i o -> p (i o)"), [[1, RUN]], base=0, channel_multiplier=RUN,
+            allow_small_or_imprecise_dtypes=True,
+        )
+        nc.gpsimd.tensor_scalar(
+            out=freq[:, 0, 0:1], in0=pos[:, 0, :], scalar1=0.0, scalar2=0.5 / math.pi, op0=ALU.mult, op1=ALU.add
         )
         w = 1
-        while w < ROPE // 2:
-            nc.vector.tensor_scalar(
-                out=freq[:, 0, w : 2 * w], in0=freq[:, 0, 0:w], scalar1=THETA ** (-2.0 * w / ROPE), scalar2=None, op0=ALU.mult
+        while w < HALF:
+            nc.gpsimd.tensor_scalar(
+                out=freq[:, 0, w : 2 * w], in0=freq[:, 0, 0:w], scalar1=THETA ** (-w / HALF), scalar2=0.0,
+                op0=ALU.mult, op1=ALU.add,
             )
             w *= 2
-        turns = keep.tile([P, RUN, ROPE // 2], F32, name="turns")
-        whole = keep.tile([P, RUN, ROPE // 2], I32, name="whole")
-        part = keep.tile([P, RUN, ROPE // 2], F32, name="part")
-        mag = keep.tile([P, RUN, ROPE // 2], F32, name="mag")
-        cos = keep.tile([P, RUN, 1, ROPE // 2], F32, name="cos")
-        sin = keep.tile([P, RUN, 2, ROPE // 2], F32, name="sin")
-        nc.vector.tensor_tensor(
-            out=turns[:],
-            in0=pos[:].unsqueeze(2).to_broadcast([P, RUN, ROPE // 2]),
-            in1=freq[:].to_broadcast([P, RUN, ROPE // 2]),
-            op=ALU.mult,
+        nc.gpsimd.tensor_tensor(
+            out=turns[:], in0=pos[:].to_broadcast([P, RUN, HALF]), in1=freq[:].to_broadcast([P, RUN, HALF]), op=ALU.mult
         )
-        nc.vector.tensor_copy(out=whole[:], in_=turns[:])
-        nc.vector.tensor_tensor(out=part[:], in0=turns[:], in1=whole[:], op=ALU.subtract)
+        nc.scalar.copy(out=xsb[:], in_=xs[:].to_broadcast([P, 2, P, 4]))
 
-        def rope_tables():
-            nc.scalar.activation(out=sin[:, :, 0, :], in_=part[:], func=ACT.Sin, scale=-2.0 * math.pi)
-            nc.scalar.activation(out=sin[:, :, 1, :], in_=part[:], func=ACT.Sin, scale=2.0 * math.pi)
-            nc.scalar.activation(out=mag[:], in_=part[:], func=ACT.Abs)
-            nc.scalar.activation(
-                out=cos[:, :, 0, :], in_=mag[:], func=ACT.Sin, scale=-2.0 * math.pi, bias=0.5 * math.pi
-            )
+        def fractions():
+            nc.vector.tensor_copy(out=whole[:], in_=turns[:])
+            nc.vector.tensor_tensor(out=part[:], in0=turns[:], in1=whole[:], op=ALU.subtract)
 
-        def permute_down():
-            nc.vector.tensor_copy(
-                out=w1[:].rearrange("p g n -> p (g n)").bitcast(I32).rearrange("p (g u q) -> p g u q", g=2, u=2),
-                in_=w1_in[:].rearrange("p g n -> p (g n)").bitcast(I32).rearrange("p (g q u) -> p g u q", g=2, u=2),
-            )
-            for g in range(2):
-                nc.vector.tensor_copy(
-                    out=w1s[:, g, :].rearrange("p (u q e) -> p u q e", u=2, e=2),
-                    in_=w1s_in[:, g, :].rearrange("p (q u e) -> p u q e", u=2, e=2),
+        def tables():
+            nc.scalar.activation(out=half_sin[:, :, 0, :], in_=part[:], func=ACT.Sin, scale=math.pi)
+            nc.scalar.activation(out=sin[:, :, 0, :], in_=part[:], func=ACT.Sin, scale=2.0 * math.pi)
+            nc.gpsimd.tensor_tensor(out=cos[:], in0=half_sin[:], in1=half_sin[:], op=ALU.mult)
+            nc.gpsimd.tensor_scalar(out=cos[:], in0=cos[:], scalar1=-2.0, scalar2=1.0, op0=ALU.mult, op1=ALU.add)
+
+        def rope_step(n):
+            q, part_of = n // 4, n % 4
+            b, i = QUAD * q // RUN, QUAD * q % RUN
+            pe = kp[:, b, i : i + QUAD]
+            if part_of == 0:
+                live["res", q] = keep.tile([P, QUAD, 4, SLOT], F32, name=f"res{q}")
+                live["by_cos"] = work.tile([P, QUAD, 2, HALF], F32, name="by_cos")
+                nc.gpsimd.tensor_tensor(
+                    out=live["by_cos"][:], in0=pe, in1=cos[:, i : i + QUAD].to_broadcast([P, QUAD, 2, HALF]), op=ALU.mult
+                )
+            elif part_of == 1:
+                live["by_sin"] = work.tile([P, QUAD, 2, HALF], F32, name="by_sin")
+                nc.gpsimd.tensor_tensor(
+                    out=live["by_sin"][:], in0=pe, in1=sin[:, i : i + QUAD].to_broadcast([P, QUAD, 2, HALF]), op=ALU.mult
+                )
+            else:
+                c = part_of - 2
+                nc.gpsimd.tensor_tensor(
+                    out=live["res", q][:, :, 0, NOPE + c * HALF : NOPE + (c + 1) * HALF],
+                    in0=live["by_cos"][:, :, c, :], in1=live["by_sin"][:, :, 1 - c, :],
+                    op=ALU.subtract if c == 0 else ALU.add,
                 )
 
-        sums = keep.tile([P, TILES], F32, name="sums")
-        rinv = keep.tile([P, TILES], F32, name="rinv")
-        live = {}
+        def closes(t):
+            return t == group_of(t)[-1]
 
-        def raw(t):
-            return xby[t // RUN][:, t % RUN, :].bitcast(FP8)
+        def slot(pool, name, t, shape, dtype, **kw):
+            g = group_of(t)
+            if t == g[0]:
+                live[name, g[0]] = pool.tile([P, len(g)] + shape, dtype, name=name, **kw)
+            return live[name, g[0]], t - g[0]
+
+        def held(name, t):
+            g = group_of(t)
+            return live[name, g[0]], t - g[0]
 
         def widen(t):
-            live["xb", t] = work.tile([P, D], BF16, name="xb", bufs=4)
+            if not closes(t):
+                return
+            g = group_of(t)
+            b, i = g[0] // RUN, g[0] % RUN
+            xb = work.tile([P, len(g), D], BF16, name="xb")
+            live["xb", g[0]] = xb
+            out = xb[:].rearrange("p j k -> p (j k)")
+            raw = xby[b][:, i : i + len(g), :].rearrange("p j k -> p (j k)").bitcast(FP8)
             if t < 2:
-                nc.vector.tensor_copy(out=live["xb", t][:], in_=raw(t))
+                nc.vector.tensor_copy(out=out, in_=raw)
             else:
-                nc.scalar.copy(out=live["xb", t][:], in_=raw(t))
+                nc.scalar.copy(out=out, in_=raw)
 
         def turn_x(t):
-            words = live.pop(("xb", t))[:].bitcast(F32)
+            xb, j = held("xb", t)
+            words = xb[:, j].bitcast(F32)
             xt = psum.tile([P, 2, 2, P], F32, name="xt", bufs=2)
             for g in range(2):
                 for u in range(2):
@@ -157,33 +201,36 @@ def tile_modelnew_pb_t_w4_kernel(
             live["xt", t] = xt
 
         def scale_x(t):
-            xg = work.tile([P, 2 * P, 4], BF16, name="xg", align_bytes=64, bufs=3)
+            xg, j = slot(work, "xg", t, [2 * P, 4], BF16, align_bytes=64)
             nc.vector.tensor_tensor(
-                out=xg[:].rearrange("p m (u e) -> p m u e", u=2),
+                out=xg[:, j].rearrange("p m (u e) -> p m u e", u=2),
                 in0=live.pop(("xt", t))[:].rearrange("p u g r -> p (u g r)").bitcast(BF16).rearrange(
                     "p (u m e) -> p m u e", u=2, e=2
                 ),
                 in1=xsb[:].rearrange("p g r (u e) -> p (g r) u e", u=2),
                 op=ALU.mult,
             )
-            live["xg", t] = xg
 
         def quant_x(t):
-            xq = work.tile([P, 2, P], U32, name="xq", align_bytes=64, bufs=3)
-            xqs = work.tile([P, 2, P], U8, name="xqs", align_bytes=64, bufs=3)
+            if not closes(t):
+                return
+            g = group_of(t)
+            xq = work.tile([P, len(g), 2, P], U32, name="xq", align_bytes=64)
+            xqs = work.tile([P, len(g), 2, P], U8, name="xqs", align_bytes=64)
             nc.vector.quantize_mx(
-                out=xq[:].rearrange("p g r -> p (g r)").bitcast(FP8X4),
-                scales=xqs[:].rearrange("p g r -> p (g r)"),
-                in_=live.pop(("xg", t))[:].rearrange("p m t -> p (m t)"),
+                out=xq[:].rearrange("p j g r -> p (j g r)").bitcast(FP8X4),
+                scales=xqs[:].rearrange("p j g r -> p (j g r)"),
+                in_=live["xg", g[0]][:].rearrange("p j m t -> p (j m t)"),
             )
-            live["xq", t] = (xq, xqs)
+            live["xq", g[0]], live["xqs", g[0]] = xq, xqs
 
         def down(t):
-            xq, xqs = live.pop(("xq", t))
+            xq, j = held("xq", t)
+            xqs, j = held("xqs", t)
             ck = psum.tile([P, KR], F32, name="ck", bufs=3)
             for g in range(2):
                 nc.tensor.matmul_mx(
-                    out=ck[:], lhsT=xq[:, g, :].bitcast(FP8X4), lhsT_scale=xqs[:, g, :],
+                    out=ck[:], lhsT=xq[:, j, g, :].bitcast(FP8X4), lhsT_scale=xqs[:, j, g, :],
                     rhs=w1[:, g, :].bitcast(FP4X4), rhs_scale=w1s[:, g, :], start=(g == 0), stop=(g == 1),
                 )
             live["ck", t] = ck
@@ -193,102 +240,85 @@ def tile_modelnew_pb_t_w4_kernel(
             nc.scalar.activation(out=junk[:], in_=live["ck", t][:], func=ACT.Square, accum_out=sums[:, t : t + 1])
 
         def inverse(t):
+            c = slice(t, t + 1)
             nc.scalar.activation(
-                out=rinv[:, t : t + 1], in_=sums[:, t : t + 1], func=ACT.Abs_reciprocal_sqrt, scale=1.0 / KR, bias=EPS
+                out=rinv[:, c], in_=sums[:, c], func=ACT.Abs_reciprocal_sqrt, scale=1.0 / KR, bias=EPS
             )
 
         def norm(t):
-            nb = work.tile([P, KR], BF16, name="nb", bufs=3)
+            nb = work.tile([P, KR], BF16, name="nb")
             nc.vector.scalar_tensor_tensor(
-                out=nb[:], in0=live.pop(("ck", t))[:], scalar=rinv[:, t : t + 1],
-                in1=gain[:].rearrange("p u q e -> p (u q e)"), op0=ALU.mult, op1=ALU.mult,
+                out=nb[:], in0=live.pop(("ck", t))[:], scalar=rinv[:, t : t + 1], in1=gain[:], op0=ALU.mult, op1=ALU.mult
             )
             live["nb", t] = nb
 
         def turn_n(t):
             words = live.pop(("nb", t))[:].bitcast(F32)
-            nt = psum.tile([P, 2, P], F32, name="nt", bufs=1)
+            nt, j = slot(psum, "nt", t, [2, P], F32, bufs=1)
             for u in range(2):
-                nc.tensor.transpose(nt[:, u], words[:, u * P : (u + 1) * P], ident[:])
-            live["nt", t] = nt
+                nc.tensor.transpose(nt[:, j, u], words[:, u : u + 255 : 2], ident[:])
 
         def empty_n(t):
-            ng = work.tile([P, 4 * P], BF16, name="ng", align_bytes=64, bufs=3)
+            if not closes(t):
+                return
+            g = group_of(t)
+            ng = work.tile([P, len(g), P, 4], BF16, name="ng", align_bytes=64)
             nc.scalar.copy(
-                out=ng[:].bitcast(F32).rearrange("p (r u) -> p r u", u=2),
-                in_=live.pop(("nt", t))[:].rearrange("p u r -> p r u"),
+                out=ng[:].rearrange("p j r t -> p (j r t)").bitcast(F32).rearrange("p (j r u) -> p j r u", j=len(g), u=2),
+                in_=live["nt", g[0]][:].rearrange("p j u r -> p j r u"),
             )
-            live["ng", t] = ng
+            live["ng", g[0]] = ng
 
         def quant_n(t):
-            nq = work.tile([P, P], U32, name="nq", align_bytes=64, bufs=3)
-            nqs = work.tile([P, P], U8, name="nqs", align_bytes=64, bufs=3)
-            nc.vector.quantize_mx(out=nq[:].bitcast(FP8X4), scales=nqs[:], in_=live.pop(("ng", t))[:])
-            live["nq", t] = (nq, nqs)
+            if not closes(t):
+                return
+            g = group_of(t)
+            nq = work.tile([P, len(g), P], U32, name="nq", align_bytes=64)
+            nqs = work.tile([P, len(g), P], U8, name="nqs", align_bytes=64)
+            nc.vector.quantize_mx(
+                out=nq[:].rearrange("p j r -> p (j r)").bitcast(FP8X4), scales=nqs[:].rearrange("p j r -> p (j r)"),
+                in_=live["ng", g[0]][:].rearrange("p j r t -> p (j r t)"),
+            )
+            live["nq", g[0]], live["nqs", g[0]] = nq, nqs
 
         def up(t):
-            nq, nqs = live.pop(("nq", t))
+            nq, j = held("nq", t)
+            nqs, j = held("nqs", t)
             kv = psum.tile([P, 4, P], F32, name="kv", bufs=2)
             nc.tensor.matmul_mx(
-                out=kv[:].rearrange("p s d -> p (s d)"), lhsT=nq[:].bitcast(FP8X4), lhsT_scale=nqs[:],
+                out=kv[:].rearrange("p s d -> p (s d)"), lhsT=nq[:, j].bitcast(FP8X4), lhsT_scale=nqs[:, j],
                 rhs=w2[:, 0, :].bitcast(FP4X4), rhs_scale=w2s[:, 0, :], start=True, stop=True,
             )
             live["kv", t] = kv
 
-        def rope(q):
-            b, i = 4 * q // RUN, 4 * q % RUN
-            res = keep.tile([P, 4, 4, SLOT], F32, name=f"res{q}")
-            live["res", q] = res
-            pe = kp[:, b, i : i + 4, :].rearrange("p i (c j) -> p i c j", c=2)
-            m1 = work.tile([P, 4, 2, ROPE // 2], F32, name="m1")
-            m2 = work.tile([P, 4, 2, ROPE // 2], F32, name="m2")
-            nc.gpsimd.tensor_tensor(
-                out=m1[:], in0=pe, in1=cos[:, i : i + 4].to_broadcast([P, 4, 2, ROPE // 2]), op=ALU.mult
-            )
-            for c in range(2):
-                nc.gpsimd.tensor_tensor(
-                    out=m2[:, :, c, :], in0=pe[:, :, 1 - c, :], in1=sin[:, i : i + 4, c, :], op=ALU.mult
-                )
-            nc.gpsimd.tensor_tensor(
-                out=res[:, :, 0, NOPE:SLOT], in0=m1[:].rearrange("p i c j -> p i (c j)"),
-                in1=m2[:].rearrange("p i c j -> p i (c j)"), op=ALU.add,
-            )
-
         def empty_kv(t):
-            nc.scalar.copy(out=live["res", t // 4][:, t % 4, :, 0:NOPE], in_=live.pop(("kv", t))[:])
+            nc.scalar.copy(out=live["res", t // QUAD][:, t % QUAD, :, 0:NOPE], in_=live.pop(("kv", t))[:])
 
         def store(t):
             if t % 2 == 0:
                 return
-            b, i, c = t // RUN, t % RUN - 1, t % 4 - 1
-            res = live["res", t // 4][:, c : c + 2]
-            keys = [key_out[b, h].rearrange("(p i) d -> p i d", i=RUN)[:, i : i + 2, :] for h in range(H)]
+            b, i, c, n = t // RUN, t % RUN - 1, t % QUAD - 1, 2
+            res = live["res", t // QUAD][:, c : c + n]
+            keys = [key_out[b, h].rearrange("(p i) d -> p i d", i=RUN)[:, i : i + n, :] for h in range(H)]
             nc.sync.dma_start(out=keys[0], in_=res[:, :, 0, :])
             nc.sync.dma_start(out=keys[1][:, :, NOPE:SLOT], in_=res[:, :, 0, NOPE:SLOT])
             nc.sync.dma_start(out=keys[1][:, :, 0:NOPE], in_=res[:, :, 2, 0:NOPE])
             for h in range(H):
                 nc.sync.dma_start(
-                    out=v_out[b, h].rearrange("(p i) d -> p i d", i=RUN)[:, i : i + 2, :],
-                    in_=res[:, :, 2 * h + 1, 0:VD],
+                    out=v_out[b, h].rearrange("(p i) d -> p i d", i=RUN)[:, i : i + n, :], in_=res[:, :, 2 * h + 1, 0:VD]
                 )
 
         steps = [
-            (widen, 0), (turn_x, 1), (quant_x, 2), (empty_kv, 9), (store, 9), (squares, 4), (scale_x, 1), (empty_n, 6),
-            (up, 8), (inverse, 4), (down, 3), (norm, 4), (turn_n, 5), (quant_n, 6),
+            (up, 10), (down, 5), (turn_x, 2), (squares, 6), (widen, 0), (norm, 7), (empty_n, 8), (inverse, 6),
+            (turn_n, 7), (quant_n, 9), (quant_x, 4), (empty_kv, 10), (store, 10), (scale_x, 3),
         ]
-        nc.gpsimd.tensor_scalar(
-            out=xsb[:], in0=xs[:].to_broadcast([P, 2, P, 4]), scalar1=1.0, scalar2=0.0, op0=ALU.mult, op1=ALU.add
-        )
-        nc.gpsimd.tensor_scalar(
-            out=gain[:], in0=gain_in[:].rearrange("p (q u e) -> p u q e", u=2, e=2), scalar1=1.0, scalar2=0.0,
-            op0=ALU.mult, op1=ALU.add,
-        )
-        rope_tables()
-        for q in range(TILES // 4):
-            rope(q)
-        for it in range(TILES + 9):
+        for it in range(TILES + 10):
             for stage, lag in steps:
                 if 0 <= it - lag < TILES:
                     stage(it - lag)
-            if it == 1:
-                permute_down()
+                if stage == widen and it == 1:
+                    fractions()
+            if it == 4:
+                tables()
+                for n in range(TILES):
+                    rope_step(n)

import math
from contextlib import ExitStack

import concourse.mybir as mybir
from concourse.masks import make_identity

B, S, D, KR = 2, 2048, 1024, 512
H, NOPE, ROPE, VD = 2, 128, 64, 128
HALF = ROPE // 2
EPS = 1e-6
THETA = 10000.0
FLOPS = 2 * B * S * (D * KR + KR * H * (NOPE + VD))

F32 = mybir.dt.float32
BF16 = mybir.dt.bfloat16
I32 = mybir.dt.int32
U32 = mybir.dt.uint32
U8 = mybir.dt.uint8
FP8 = mybir.dt.float8_e4m3fn
FP8X4 = mybir.dt.float8_e4m3fn_x4
FP4X4 = mybir.dt.float4_e2m1fn_x4
ACT = mybir.ActivationFunctionType
ALU = mybir.AluOpType

P = 128
RUN = S // P
TILES = B * RUN
SLOT = NOPE + ROPE
QUAD = 4


def group_of(t):
    return [t]


def tile_modelnew_pb_t_w4_kernel(
    tc, x_bytes, x_scale, w1_words, w1_scales, k_pe_raw, ln_w, w2_words, w2_scales, key_out, v_out
):
    nc = tc.nc
    with ExitStack() as ctx:
        keep = ctx.enter_context(tc.tile_pool(name="keep", bufs=1))
        work = ctx.enter_context(tc.tile_pool(name="work", bufs=4))
        psum = ctx.enter_context(tc.psum_pool(name="psum", bufs=1))
        ctx.enter_context(tc.manual_schedule())

        xby = [keep.tile([P, RUN, D], U8, name=f"xby{b}") for b in range(B)]
        xs = keep.tile([P, 2, 1, 4], F32, name="xs")
        xsb = keep.tile([P, 2, P, 4], F32, name="xsb")
        w1 = keep.tile([P, 2, 2 * KR], U8, name="w1", align_bytes=64)
        w1s = keep.tile([P, 2, KR], U8, name="w1s", align_bytes=64)
        w2 = keep.tile([P, 1, 2 * KR], U8, name="w2", align_bytes=64)
        w2s = keep.tile([P, 1, KR], U8, name="w2s", align_bytes=64)
        gain = keep.tile([P, KR], BF16, name="gain")
        kp = keep.tile([P, B, RUN, 2, HALF], BF16, name="kp")
        ident = keep.tile([P, P], F32, name="ident")
        zero = keep.tile([P, 1], F32, name="zero")
        spare = keep.tile([P, 1], F32, name="spare")
        pos = keep.tile([P, RUN, 1], F32, name="pos")
        freq = keep.tile([P, 1, HALF], F32, name="freq")
        turns = keep.tile([P, RUN, HALF], F32, name="turns")
        whole = keep.tile([P, RUN, HALF], I32, name="whole")
        part = keep.tile([P, RUN, HALF], F32, name="part")
        sin = keep.tile([P, RUN, 1, HALF], F32, name="sin")
        half_sin = keep.tile([P, RUN, 1, HALF], F32, name="half_sin")
        cos = keep.tile([P, RUN, 1, HALF], F32, name="cos")
        sums = keep.tile([P, TILES], F32, name="sums")
        rinv = keep.tile([P, TILES], F32, name="rinv")
        live = {}

        nc.vector.memset(w1s[:].rearrange("p g n -> p (g n)").bitcast(I32), 0)
        nc.vector.memset(zero[:], 0.0)
        nc.vector.memset(w2s[:].rearrange("p g n -> p (g n)").bitcast(I32), 0)
        nc.scalar.activation(out=spare[:], in_=zero[:], func=ACT.Sin)

        def load_x(b, i0, i1):
            nc.sync.dma_start(
                out=xby[b][:, i0:i1, :], in_=x_bytes[b].rearrange("(p i) k -> p i k", i=RUN)[:, i0:i1, :]
            )

        def load_scales(tile, dram):
            for q in range(4):
                nc.sync.dma_start(
                    out=tile[32 * q : 32 * q + 4, :, :].bitcast(I32),
                    in_=dram[:, 4 * q : 4 * q + 4, :].rearrange("g q n -> q g n").bitcast(I32),
                )

        def load_rope_key(b):
            nc.sync.dma_start(
                out=kp[:, b].rearrange("p i c j -> p i (c j)"), in_=k_pe_raw[b].rearrange("(p i) d -> p i d", i=RUN)
            )

        load_x(0, 0, 1)
        nc.sync.dma_start(
            out=xs[:].rearrange("p g o t -> p (g o) t"),
            in_=x_scale.rearrange("a b (g p t) -> p (a b g) t", p=P, t=4),
        )
        load_x(0, 1, 2)
        nc.sync.dma_start(out=w1[:], in_=w1_words.rearrange("g p n -> p g n"))
        load_scales(w1s, w1_scales)
        load_x(0, 2, 4)
        load_x(0, 4, 8)
        nc.sync.dma_start(out=gain[:], in_=ln_w.partition_broadcast(P))
        load_rope_key(0)
        load_scales(w2s, w2_scales)
        nc.sync.dma_start(out=w2[:], in_=w2_words.rearrange("g p n -> p g n"))
        load_x(0, 8, 12)
        load_x(0, 12, 16)
        load_x(1, 0, 4)
        load_rope_key(1)
        for i in range(4, RUN, 4):
            load_x(1, i, i + 4)

        make_identity(nc, ident[:])
        nc.gpsimd.iota(
            pos[:].rearrange("p i o -> p (i o)"), [[1, RUN]], base=0, channel_multiplier=RUN,
            allow_small_or_imprecise_dtypes=True,
        )
        nc.gpsimd.tensor_scalar(
            out=freq[:, 0, 0:1], in0=pos[:, 0, :], scalar1=0.0, scalar2=0.5 / math.pi, op0=ALU.mult, op1=ALU.add
        )
        w = 1
        while w < HALF:
            nc.gpsimd.tensor_scalar(
                out=freq[:, 0, w : 2 * w], in0=freq[:, 0, 0:w], scalar1=THETA ** (-w / HALF), scalar2=0.0,
                op0=ALU.mult, op1=ALU.add,
            )
            w *= 2
        nc.gpsimd.tensor_tensor(
            out=turns[:], in0=pos[:].to_broadcast([P, RUN, HALF]), in1=freq[:].to_broadcast([P, RUN, HALF]), op=ALU.mult
        )
        nc.scalar.copy(out=xsb[:], in_=xs[:].to_broadcast([P, 2, P, 4]))

        def fractions():
            nc.vector.tensor_copy(out=whole[:], in_=turns[:])
            nc.vector.tensor_tensor(out=part[:], in0=turns[:], in1=whole[:], op=ALU.subtract)

        def tables():
            nc.scalar.activation(out=half_sin[:, :, 0, :], in_=part[:], func=ACT.Sin, scale=math.pi)
            nc.scalar.activation(out=sin[:, :, 0, :], in_=part[:], func=ACT.Sin, scale=2.0 * math.pi)
            nc.gpsimd.tensor_tensor(out=cos[:], in0=half_sin[:], in1=half_sin[:], op=ALU.mult)
            nc.gpsimd.tensor_scalar(out=cos[:], in0=cos[:], scalar1=-2.0, scalar2=1.0, op0=ALU.mult, op1=ALU.add)

        def rope_step(n):
            q, part_of = n // 4, n % 4
            b, i = QUAD * q // RUN, QUAD * q % RUN
            pe = kp[:, b, i : i + QUAD]
            if part_of == 0:
                live["res", q] = keep.tile([P, QUAD, 4, SLOT], F32, name=f"res{q}")
                live["by_cos"] = work.tile([P, QUAD, 2, HALF], F32, name="by_cos")
                nc.gpsimd.tensor_tensor(
                    out=live["by_cos"][:], in0=pe, in1=cos[:, i : i + QUAD].to_broadcast([P, QUAD, 2, HALF]), op=ALU.mult
                )
            elif part_of == 1:
                live["by_sin"] = work.tile([P, QUAD, 2, HALF], F32, name="by_sin")
                nc.gpsimd.tensor_tensor(
                    out=live["by_sin"][:], in0=pe, in1=sin[:, i : i + QUAD].to_broadcast([P, QUAD, 2, HALF]), op=ALU.mult
                )
            else:
                c = part_of - 2
                nc.gpsimd.tensor_tensor(
                    out=live["res", q][:, :, 0, NOPE + c * HALF : NOPE + (c + 1) * HALF],
                    in0=live["by_cos"][:, :, c, :], in1=live["by_sin"][:, :, 1 - c, :],
                    op=ALU.subtract if c == 0 else ALU.add,
                )

        def closes(t):
            return t == group_of(t)[-1]

        def slot(pool, name, t, shape, dtype, **kw):
            g = group_of(t)
            if t == g[0]:
                live[name, g[0]] = pool.tile([P, len(g)] + shape, dtype, name=name, **kw)
            return live[name, g[0]], t - g[0]

        def held(name, t):
            g = group_of(t)
            return live[name, g[0]], t - g[0]

        def widen(t):
            if not closes(t):
                return
            g = group_of(t)
            b, i = g[0] // RUN, g[0] % RUN
            xb = work.tile([P, len(g), D], BF16, name="xb")
            live["xb", g[0]] = xb
            out = xb[:].rearrange("p j k -> p (j k)")
            raw = xby[b][:, i : i + len(g), :].rearrange("p j k -> p (j k)").bitcast(FP8)
            if t < 2:
                nc.vector.tensor_copy(out=out, in_=raw)
            else:
                nc.scalar.copy(out=out, in_=raw)

        def turn_x(t):
            xb, j = held("xb", t)
            words = xb[:, j].bitcast(F32)
            xt = psum.tile([P, 2, 2, P], F32, name="xt", bufs=2)
            for g in range(2):
                for u in range(2):
                    c = g * 256 + u
                    nc.tensor.transpose(xt[:, u, g], words[:, c : c + 255 : 2], ident[:])
            live["xt", t] = xt

        def scale_x(t):
            xg, j = slot(work, "xg", t, [2 * P, 4], BF16, align_bytes=64)
            nc.vector.tensor_tensor(
                out=xg[:, j].rearrange("p m (u e) -> p m u e", u=2),
                in0=live.pop(("xt", t))[:].rearrange("p u g r -> p (u g r)").bitcast(BF16).rearrange(
                    "p (u m e) -> p m u e", u=2, e=2
                ),
                in1=xsb[:].rearrange("p g r (u e) -> p (g r) u e", u=2),
                op=ALU.mult,
            )

        def quant_x(t):
            if not closes(t):
                return
            g = group_of(t)
            xq = work.tile([P, len(g), 2, P], U32, name="xq", align_bytes=64)
            xqs = work.tile([P, len(g), 2, P], U8, name="xqs", align_bytes=64)
            nc.vector.quantize_mx(
                out=xq[:].rearrange("p j g r -> p (j g r)").bitcast(FP8X4),
                scales=xqs[:].rearrange("p j g r -> p (j g r)"),
                in_=live["xg", g[0]][:].rearrange("p j m t -> p (j m t)"),
            )
            live["xq", g[0]], live["xqs", g[0]] = xq, xqs

        def down(t):
            xq, j = held("xq", t)
            xqs, j = held("xqs", t)
            ck = psum.tile([P, KR], F32, name="ck", bufs=3)
            for g in range(2):
                nc.tensor.matmul_mx(
                    out=ck[:], lhsT=xq[:, j, g, :].bitcast(FP8X4), lhsT_scale=xqs[:, j, g, :],
                    rhs=w1[:, g, :].bitcast(FP4X4), rhs_scale=w1s[:, g, :], start=(g == 0), stop=(g == 1),
                )
            live["ck", t] = ck

        def squares(t):
            junk = work.tile([P, KR], BF16, name="junk")
            nc.scalar.activation(out=junk[:], in_=live["ck", t][:], func=ACT.Square, accum_out=sums[:, t : t + 1])

        def inverse(t):
            c = slice(t, t + 1)
            nc.scalar.activation(
                out=rinv[:, c], in_=sums[:, c], func=ACT.Abs_reciprocal_sqrt, scale=1.0 / KR, bias=EPS
            )

        def norm(t):
            nb = work.tile([P, KR], BF16, name="nb")
            nc.vector.scalar_tensor_tensor(
                out=nb[:], in0=live.pop(("ck", t))[:], scalar=rinv[:, t : t + 1], in1=gain[:], op0=ALU.mult, op1=ALU.mult
            )
            live["nb", t] = nb

        def turn_n(t):
            words = live.pop(("nb", t))[:].bitcast(F32)
            nt, j = slot(psum, "nt", t, [2, P], F32, bufs=1)
            for u in range(2):
                nc.tensor.transpose(nt[:, j, u], words[:, u : u + 255 : 2], ident[:])

        def empty_n(t):
            if not closes(t):
                return
            g = group_of(t)
            ng = work.tile([P, len(g), P, 4], BF16, name="ng", align_bytes=64)
            nc.scalar.copy(
                out=ng[:].rearrange("p j r t -> p (j r t)").bitcast(F32).rearrange("p (j r u) -> p j r u", j=len(g), u=2),
                in_=live["nt", g[0]][:].rearrange("p j u r -> p j r u"),
            )
            live["ng", g[0]] = ng

        def quant_n(t):
            if not closes(t):
                return
            g = group_of(t)
            nq = work.tile([P, len(g), P], U32, name="nq", align_bytes=64)
            nqs = work.tile([P, len(g), P], U8, name="nqs", align_bytes=64)
            nc.vector.quantize_mx(
                out=nq[:].rearrange("p j r -> p (j r)").bitcast(FP8X4), scales=nqs[:].rearrange("p j r -> p (j r)"),
                in_=live["ng", g[0]][:].rearrange("p j r t -> p (j r t)"),
            )
            live["nq", g[0]], live["nqs", g[0]] = nq, nqs

        def up(t):
            nq, j = held("nq", t)
            nqs, j = held("nqs", t)
            kv = psum.tile([P, 4, P], F32, name="kv", bufs=2)
            nc.tensor.matmul_mx(
                out=kv[:].rearrange("p s d -> p (s d)"), lhsT=nq[:, j].bitcast(FP8X4), lhsT_scale=nqs[:, j],
                rhs=w2[:, 0, :].bitcast(FP4X4), rhs_scale=w2s[:, 0, :], start=True, stop=True,
            )
            live["kv", t] = kv

        def empty_kv(t):
            nc.scalar.copy(out=live["res", t // QUAD][:, t % QUAD, :, 0:NOPE], in_=live.pop(("kv", t))[:])

        def store(t):
            if t % 2 == 0:
                return
            b, i, c, n = t // RUN, t % RUN - 1, t % QUAD - 1, 2
            res = live["res", t // QUAD][:, c : c + n]
            keys = [key_out[b, h].rearrange("(p i) d -> p i d", i=RUN)[:, i : i + n, :] for h in range(H)]
            nc.sync.dma_start(out=keys[0], in_=res[:, :, 0, :])
            nc.sync.dma_start(out=keys[1][:, :, NOPE:SLOT], in_=res[:, :, 0, NOPE:SLOT])
            nc.sync.dma_start(out=keys[1][:, :, 0:NOPE], in_=res[:, :, 2, 0:NOPE])
            for h in range(H):
                nc.sync.dma_start(
                    out=v_out[b, h].rearrange("(p i) d -> p i d", i=RUN)[:, i : i + n, :], in_=res[:, :, 2 * h + 1, 0:VD]
                )

        steps = [
            (up, 10), (down, 5), (turn_x, 2), (squares, 6), (widen, 0), (norm, 7), (empty_n, 8), (inverse, 6),
            (turn_n, 7), (quant_n, 9), (quant_x, 4), (empty_kv, 10), (store, 10), (scale_x, 3),
        ]
        for it in range(TILES + 10):
            for stage, lag in steps:
                if 0 <= it - lag < TILES:
                    stage(it - lag)
                if stage == widen and it == 1:
                    fractions()
            if it == 4:
                tables()
                for n in range(TILES):
                    rope_step(n)
